import numpy as np
import ml_dtypes


def mxq(x, axis, fmt="e4m3"):
    dtype, down = {"e4m3": (ml_dtypes.float8_e4m3fn, 7), "e5m2": (ml_dtypes.float8_e5m2, 14)}[fmt]
    v = np.moveaxis(np.asarray(x, np.float32).astype(ml_dtypes.bfloat16).astype(np.float64), axis, -1)
    blocks = v.reshape(v.shape[:-1] + (-1, 32))
    amax = np.abs(blocks).max(-1, keepdims=True)
    byte = np.maximum(np.where(amax > 0, np.frexp(amax)[1] - 1 + 127, 0) - down, 1)
    scale = np.exp2(byte - 127.0)
    codes = (blocks / scale).astype(np.float32).astype(dtype).astype(np.float64)
    return np.moveaxis((codes * scale).reshape(v.shape), -1, axis)


WIDE = False


def mx_kscale(k):
    if not WIDE:
        return np.ones(k)
    levels = np.array([10, -10, 5, -5, 0])
    a = np.random.permutation(np.resize(levels, k // 512 * 4)).reshape(k // 512, 4)
    idx = np.arange(k)
    return np.exp2(a[idx // 512, idx % 128 // 32])


BF16 = ml_dtypes.bfloat16


def bf(x):
    return np.asarray(x, np.float32).astype(BF16)


def f64(x):
    return np.asarray(x).astype(np.float64)


E2M1 = np.array([0.0, 0.5, 1.0, 1.5, 2.0, 3.0, 4.0, 6.0, -0.0, -0.5, -1.0, -1.5, -2.0, -3.0, -4.0, -6.0])


def pack_weight(w, fmt):
    k, n = w.shape
    w = f64(bf(w)).reshape(k // 32, 32, n)
    amax = np.abs(w).max(1)
    if fmt == "e4m3":
        byte = np.frexp(amax)[1] - 1 + 127 - 7
    else:
        mant, ex = np.frexp(amax / 6.0)
        byte = np.where(mant > 0.5, ex, ex - 1) + 127
    byte = np.clip(np.where(amax > 0, byte, 1), 1, 254)
    scaled = (w * np.exp2(127.0 - byte)[:, None, :]).reshape(k, n).astype(np.float32)
    by_word = np.ascontiguousarray(scaled.reshape(k // 512, 128, 4, n).transpose(0, 1, 3, 2))
    if fmt == "e4m3":
        words = by_word.astype(ml_dtypes.float8_e4m3fn).view(np.uint8)
    else:
        c = by_word.astype(ml_dtypes.float4_e2m1fn).view(np.uint8) & 0xF
        words = c[..., 0::2] | (c[..., 1::2] << 4)
    return np.ascontiguousarray(words), np.ascontiguousarray(byte.astype(np.uint8).reshape(k // 512, 16, n))


def unpack_weight(words, scales, fmt):
    g, p, n, _ = words.shape
    if fmt == "e4m3":
        vals = np.ascontiguousarray(words).view(ml_dtypes.float8_e4m3fn).astype(np.float64)
    else:
        nib = np.empty((g, p, n, 4), np.uint8)
        nib[..., 0::2] = words & 0xF
        nib[..., 1::2] = words >> 4
        vals = E2M1[nib]
    vals = vals * np.repeat(np.exp2(scales.astype(np.float64) - 127.0), 8, axis=1)[..., None]
    return vals.transpose(0, 1, 3, 2).reshape(g * 512, n)

def pack4(w):
    words, scales = pack_weight(w, "e2m1")
    return words.reshape(words.shape[0], 128, -1), scales


def unpack4(words, scales):
    return unpack_weight(words.reshape(words.shape[0], 128, -1, 2), scales, "e2m1")


B, C, W, H = 8, 512, 16, 32


def spatial_shift1(y):
    cq = y.shape[-1] // 4
    p0 = np.concatenate([y[:, :1, :, 0 * cq:1 * cq], y[:, :-1, :, 0 * cq:1 * cq]], axis=1)
    p1 = np.concatenate([y[:, 1:, :, 1 * cq:2 * cq], y[:, -1:, :, 1 * cq:2 * cq]], axis=1)
    p2 = np.concatenate([y[:, :, :1, 2 * cq:3 * cq], y[:, :, :-1, 2 * cq:3 * cq]], axis=2)
    p3 = np.concatenate([y[:, :, 1:, 3 * cq:], y[:, :, -1:, 3 * cq:]], axis=2)
    return np.concatenate([p0, p1, p2, p3], axis=-1)


def spatial_shift2(y):
    cq = y.shape[-1] // 4
    p0 = np.concatenate([y[:, :, :1, 0 * cq:1 * cq], y[:, :, :-1, 0 * cq:1 * cq]], axis=2)
    p1 = np.concatenate([y[:, :, 1:, 1 * cq:2 * cq], y[:, :, -1:, 1 * cq:2 * cq]], axis=2)
    p2 = np.concatenate([y[:, :1, :, 2 * cq:3 * cq], y[:, :-1, :, 2 * cq:3 * cq]], axis=1)
    p3 = np.concatenate([y[:, 1:, :, 3 * cq:], y[:, -1:, :, 3 * cq:]], axis=1)
    return np.concatenate([p0, p1, p2, p3], axis=-1)


def setup_inputs():
    s = mx_kscale(C)
    x = bf(np.random.standard_normal((B, C, W, H)) * s[None, :, None, None])
    w1 = np.random.standard_normal((3 * C, C)) / np.sqrt(C) / s[None, :]
    w1_words, w1_scales = pack4(np.ascontiguousarray(w1.T))
    b1 = bf(np.random.standard_normal(3 * C) * 0.1)
    return {"x": x, "w1_words": w1_words, "w1_scales": w1_scales, "b1": b1}


def reference(x, w1_words, w1_scales, b1):
    xp = f64(x).transpose(0, 2, 3, 1)
    y = (mxq(xp, 3, "e4m3") @ unpack4(w1_words, w1_scales)) + f64(b1)
    x1 = spatial_shift1(y[..., :C])
    x2 = spatial_shift2(y[..., C:2 * C])
    x3 = y[..., 2 * C:]
    a = np.sum(x1 + x2 + x3, axis=(1, 2))
    return x1, x2, x3, a

@@ -1,0 +1,199 @@
+from contextlib import ExitStack
+
+import concourse.mybir as mybir
+from concourse.masks import make_identity
+
+BF16 = mybir.dt.bfloat16
+F32 = mybir.dt.float32
+I32 = mybir.dt.int32
+U32 = mybir.dt.uint32
+U8 = mybir.dt.uint8
+FP8X4 = mybir.dt.float8_e4m3fn_x4
+FP4X4 = mybir.dt.float4_e2m1fn_x4
+ADD = mybir.AluOpType.add
+
+B, C, W, H = 8, 512, 16, 32
+P = 128
+PACK = 4
+QUARTER = C // 4
+BRANCHES = 3
+FLOPS = 2 * B * W * H * C * BRANCHES * C
+
+SAME, W_MINUS, W_PLUS, H_MINUS, H_PLUS = 0, 1, 2, 3, 4
+X1_SHIFTS = (W_MINUS, W_PLUS, H_MINUS, H_PLUS)
+X2_SHIFTS = (H_MINUS, H_PLUS, W_MINUS, W_PLUS)
+
+RUN = 4
+ROWS_PER_QUANTISE = 4
+ROWS_PER_STORE = 2
+
+
+def branch_pieces(branch):
+    if branch == 0:
+        return [(s, q * QUARTER, QUARTER) for q, s in enumerate(X1_SHIFTS)]
+    if branch == 1:
+        return [(s, C + q * QUARTER, QUARTER) for q, s in enumerate(X2_SHIFTS)]
+    return [(SAME, 2 * C, C)]
+
+
+def tile_modelnew_pa_t_kernel(tc, x, w1_words, w1_scales, b1, out_0, out_1, out_2, out_3):
+    nc = tc.nc
+    outs = (out_0, out_1, out_2)
+    with ExitStack() as ctx:
+        keep = ctx.enter_context(tc.tile_pool(name="keep", bufs=1))
+        loads = ctx.enter_context(tc.tile_pool(name="loads", bufs=B // 2))
+        results = ctx.enter_context(tc.tile_pool(name="results", bufs=3))
+        banks = ctx.enter_context(tc.psum_pool(name="banks", bufs=7))
+        pooled = ctx.enter_context(tc.psum_pool(name="pooled", bufs=1))
+
+        w_words = keep.tile([P, 2 * BRANCHES * C], U8, align_bytes=64)
+        w_plane = keep.tile([P, BRANCHES * C], U8, align_bytes=64)
+        nc.vector.memset(w_plane[:].bitcast(I32), 0)
+        for quadrant in range(4):
+            nc.sync.dma_start(
+                out=w_plane[32 * quadrant : 32 * quadrant + 4, :].bitcast(I32),
+                in_=w1_scales[0, 4 * quadrant : 4 * quadrant + 4, :].bitcast(I32),
+            )
+        nc.sync.dma_start(out=w_words[:].bitcast(I32), in_=w1_words[0].bitcast(I32))
+
+        bias_row = keep.tile([P, BRANCHES * C], BF16)
+        nc.vector.memset(bias_row[:], 0.0)
+        nc.sync.dma_start(out=bias_row[0:1, :], in_=b1.rearrange("(o n) -> o n", o=1))
+
+        raw = []
+        for pair in range(B // 2):
+            raw_pair = loads.tile([P, 2, PACK * W * H], BF16, name="raw_pair")
+            nc.sync.dma_start(
+                out=raw_pair[:],
+                in_=x[2 * pair : 2 * pair + 2].rearrange("b (p j) w h -> p b (j w h)", j=PACK),
+            )
+            raw.append(raw_pair)
+
+        ones = keep.tile([P, P], BF16)
+        nc.vector.memset(ones[:], 1.0)
+        bias = keep.tile([P, BRANCHES * C], F32)
+        for branch in range(BRANCHES):
+            cols = slice(branch * C, (branch + 1) * C)
+            spread = banks.tile([P, C], F32, name="bank")
+            nc.tensor.matmul(out=spread[:], lhsT=ones[:], rhs=bias_row[:, cols], start=True, stop=True)
+            nc.scalar.copy(out=bias[:, cols], in_=spread[:])
+        bias_pooled = keep.tile([P, C], F32)
+        nc.vector.tensor_tensor(out=bias_pooled[:], in0=bias[:, 0:C], in1=bias[:, C : 2 * C], op=ADD)
+        nc.vector.tensor_tensor(out=bias_pooled[:], in0=bias_pooled[:], in1=bias[:, 2 * C : 3 * C], op=ADD)
+        nc.vector.tensor_scalar_mul(out=bias_pooled[:], in0=bias_pooled[:], scalar1=float(W * H))
+
+        identity = keep.tile([P, P], F32)
+        make_identity(nc, identity[:])
+        same_batch = keep.tile([P, P], F32)
+        nc.vector.memset(same_batch[:], 0.0)
+        nc.vector.tensor_reduce(
+            out=same_batch[:, 0:B],
+            in_=identity[:].rearrange("p (w b) -> p b w", b=B),
+            axis=mybir.AxisListType.X,
+            op=ADD,
+        )
+
+        grouped = keep.tile([P, H, W, B * PACK], BF16, align_bytes=64)
+        for pair in range(B // 2):
+            by_channel = raw[pair][:].rearrange("p b (j w h) -> p (b j) w h", j=PACK, w=W)
+            cols = slice(2 * PACK * pair, 2 * PACK * (pair + 1))
+            for first_row in range(0, H, RUN):
+                rows = slice(first_row, first_row + RUN)
+                src = by_channel[:, :, :, rows].rearrange("p c w i -> p w c i")
+                dst = grouped[:, rows, :, cols].rearrange("p i w c -> p w c i")
+                if first_row < H // 2:
+                    nc.vector.tensor_copy(out=dst, in_=src)
+                else:
+                    nc.scalar.copy(out=dst, in_=src)
+
+        words = {}
+        planes = {}
+        for shift in (SAME, W_MINUS, W_PLUS):
+            words[shift] = keep.tile([P, H, P], U32, name="words%d" % shift, align_bytes=64)
+            planes[shift] = keep.tile([P, H, P], U8, name="planes%d" % shift, align_bytes=64)
+        nc.vector.memset(planes[SAME][:].bitcast(I32), 0)
+
+        def quantise(first_row):
+            rows = slice(first_row, first_row + ROWS_PER_QUANTISE)
+            nc.vector.quantize_mx(
+                out=words[SAME][:, rows, :].rearrange("p r m -> p (r m)").bitcast(FP8X4),
+                scales=planes[SAME][:, rows, :].rearrange("p r m -> p (r m)"),
+                in_=grouped[:, rows, :, :].rearrange("p r w c -> p (r w c)"),
+            )
+
+        def move_in_w(tiles, rows, step):
+            same = tiles[SAME][:].bitcast(I32)
+            minus = tiles[W_MINUS][:].bitcast(I32)
+            plus = tiles[W_PLUS][:].bitcast(I32)
+            n = same.shape[2]
+            nc.vector.tensor_copy(out=minus[:, rows, step:n], in_=same[:, rows, 0 : n - step])
+            nc.vector.tensor_copy(out=minus[:, rows, 0:step], in_=same[:, rows, 0:step])
+            nc.vector.tensor_copy(out=plus[:, rows, 0 : n - step], in_=same[:, rows, step:n])
+            nc.vector.tensor_copy(out=plus[:, rows, n - step : n], in_=same[:, rows, n - step : n])
+
+        def prepare(first_row):
+            quantise(first_row)
+            rows = slice(first_row, first_row + ROWS_PER_QUANTISE)
+            move_in_w(words, rows, B)
+            move_in_w(planes, rows, B // 4)
+
+        def project(out, shift, h, first, width, start, stop):
+            if shift == H_MINUS:
+                source, row = SAME, max(h - 1, 0)
+            elif shift == H_PLUS:
+                source, row = SAME, min(h + 1, H - 1)
+            else:
+                source, row = shift, h
+            nc.tensor.matmul_mx(
+                out=out,
+                lhsT=words[source][:, row, :].bitcast(FP8X4),
+                lhsT_scale=planes[source][:, row, :],
+                rhs=w_words[:, 2 * first : 2 * (first + width)].bitcast(FP4X4),
+                rhs_scale=w_plane[:, first : first + width],
+                start=start,
+                stop=stop,
+            )
+
+        pooled_sum = pooled.tile([P, C], F32)
+        branch_order = (2, 0, 1)
+        prepare(0)
+        rows_out = {}
+        for h in range(H):
+            if h % ROWS_PER_QUANTISE == 0 and h + ROWS_PER_QUANTISE < H:
+                prepare(h + ROWS_PER_QUANTISE)
+            slot = h % ROWS_PER_STORE
+            for branch in branch_order:
+                if slot == 0:
+                    rows_out[branch] = results.tile([P, ROWS_PER_STORE, C], F32, name="rows%d" % branch)
+                bank = banks.tile([P, C], F32, name="bank")
+                for shift, first, width in branch_pieces(branch):
+                    at = first - branch * C
+                    project(bank[:, at : at + width], shift, h, first, width, True, True)
+                row = rows_out[branch][:, slot, :]
+                bias_cols = bias[:, branch * C : (branch + 1) * C]
+                if branch == 2:
+                    nc.scalar.copy(out=row, in_=bank[:])
+                    nc.gpsimd.tensor_tensor(out=row, in0=row, in1=bias_cols, op=ADD)
+                else:
+                    nc.vector.tensor_tensor(out=row, in0=bank[:], in1=bias_cols, op=ADD)
+            for branch in branch_order:
+                for shift, first, width in branch_pieces(branch):
+                    at = first - branch * C
+                    opens = h == 0 and branch == branch_order[0]
+                    closes = h == H - 1 and first + width == 2 * C
+                    project(pooled_sum[:, at : at + width], shift, h, first, width, opens, closes)
+            if slot == ROWS_PER_STORE - 1:
+                first_row = h - slot
+                for branch in branch_order:
+                    nc.sync.dma_start(
+                        out=outs[branch].rearrange("b w h c -> w b (h c)")[:, :, first_row * C : (h + 1) * C],
+                        in_=rows_out[branch][:].rearrange("p r c -> p (r c)"),
+                    )
+
+        by_point = keep.tile([P, C], F32)
+        nc.vector.tensor_copy(out=by_point[:], in_=pooled_sum[:])
+        by_batch = banks.tile([P, C], F32, name="bank")
+        nc.tensor.matmul(out=by_batch[:], lhsT=same_batch[:], rhs=by_point[:], start=True, stop=True)
+        a_rows = keep.tile([P, C], F32)
+        nc.vector.tensor_tensor(out=a_rows[:], in0=by_batch[:], in1=bias_pooled[:], op=ADD)
+        nc.sync.dma_start(out=out_3, in_=a_rows[0:B, :])

@@ -26,6 +26,7 @@ X2_SHIFTS = (H_MINUS, H_PLUS, W_MINUS, W_PLUS)
 RUN = 4
 ROWS_PER_QUANTISE = 4
 ROWS_PER_STORE = 2
+GROUPS_BEFORE_LOOP = 3
 
 
 def branch_pieces(branch):
@@ -40,9 +41,10 @@ def tile_modelnew_pa_t_kernel(tc, x, w1_words, w1_scales, b1, out_0, out_1, out_
     nc = tc.nc
     outs = (out_0, out_1, out_2)
     with ExitStack() as ctx:
+        ctx.enter_context(tc.manual_schedule())
         keep = ctx.enter_context(tc.tile_pool(name="keep", bufs=1))
         loads = ctx.enter_context(tc.tile_pool(name="loads", bufs=B // 2))
-        results = ctx.enter_context(tc.tile_pool(name="results", bufs=3))
+        results = ctx.enter_context(tc.tile_pool(name="results", bufs=4))
         banks = ctx.enter_context(tc.psum_pool(name="banks", bufs=7))
         pooled = ctx.enter_context(tc.psum_pool(name="pooled", bufs=1))
 
@@ -77,10 +79,16 @@ def tile_modelnew_pa_t_kernel(tc, x, w1_words, w1_scales, b1, out_0, out_1, out_
             spread = banks.tile([P, C], F32, name="bank")
             nc.tensor.matmul(out=spread[:], lhsT=ones[:], rhs=bias_row[:, cols], start=True, stop=True)
             nc.scalar.copy(out=bias[:, cols], in_=spread[:])
+        h_fold = keep.tile([P, P], BF16)
+        nc.vector.memset(h_fold[:], float(H))
         bias_pooled = keep.tile([P, C], F32)
-        nc.vector.tensor_tensor(out=bias_pooled[:], in0=bias[:, 0:C], in1=bias[:, C : 2 * C], op=ADD)
-        nc.vector.tensor_tensor(out=bias_pooled[:], in0=bias_pooled[:], in1=bias[:, 2 * C : 3 * C], op=ADD)
-        nc.vector.tensor_scalar_mul(out=bias_pooled[:], in0=bias_pooled[:], scalar1=float(W * H))
+        spread = banks.tile([P, C], F32, name="bank")
+        for branch in range(BRANCHES):
+            cols = slice(branch * C, (branch + 1) * C)
+            nc.tensor.matmul(
+                out=spread[:], lhsT=h_fold[:], rhs=bias_row[:, cols], start=branch == 0, stop=branch == BRANCHES - 1
+            )
+        nc.scalar.copy(out=bias_pooled[:], in_=spread[:])
 
         identity = keep.tile([P, P], F32)
         make_identity(nc, identity[:])
@@ -93,25 +101,28 @@ def tile_modelnew_pa_t_kernel(tc, x, w1_words, w1_scales, b1, out_0, out_1, out_
             op=ADD,
         )
 
-        grouped = keep.tile([P, H, W, B * PACK], BF16, align_bytes=64)
-        for pair in range(B // 2):
-            by_channel = raw[pair][:].rearrange("p b (j w h) -> p (b j) w h", j=PACK, w=W)
-            cols = slice(2 * PACK * pair, 2 * PACK * (pair + 1))
-            for first_row in range(0, H, RUN):
-                rows = slice(first_row, first_row + RUN)
-                src = by_channel[:, :, :, rows].rearrange("p c w i -> p w c i")
-                dst = grouped[:, rows, :, cols].rearrange("p i w c -> p w c i")
-                if first_row < H // 2:
-                    nc.vector.tensor_copy(out=dst, in_=src)
-                else:
-                    nc.scalar.copy(out=dst, in_=src)
-
         words = {}
         planes = {}
         for shift in (SAME, W_MINUS, W_PLUS):
             words[shift] = keep.tile([P, H, P], U32, name="words%d" % shift, align_bytes=64)
             planes[shift] = keep.tile([P, H, P], U8, name="planes%d" % shift, align_bytes=64)
         nc.vector.memset(planes[SAME][:].bitcast(I32), 0)
+
+        grouped = keep.tile([P, H, W, B * PACK], BF16, align_bytes=64)
+
+        def regroup(copy, pair, group):
+            by_channel = raw[pair][:].rearrange("p b (j w h) -> p (b j) w h", j=PACK, w=W)
+            cols = slice(2 * PACK * pair, 2 * PACK * (pair + 1))
+            rows = slice(RUN * group, RUN * (group + 1))
+            copy(
+                out=grouped[:, rows, :, cols].rearrange("p i w c -> p w c i"),
+                in_=by_channel[:, :, :, rows].rearrange("p c w i -> p w c i"),
+            )
+
+        for pair in range(B // 2):
+            for group in range(GROUPS_BEFORE_LOOP):
+                regroup(nc.vector.tensor_copy, pair, group)
+
 
         def quantise(first_row):
             rows = slice(first_row, first_row + ROWS_PER_QUANTISE)
@@ -159,8 +170,6 @@ def tile_modelnew_pa_t_kernel(tc, x, w1_words, w1_scales, b1, out_0, out_1, out_
         prepare(0)
         rows_out = {}
         for h in range(H):
-            if h % ROWS_PER_QUANTISE == 0 and h + ROWS_PER_QUANTISE < H:
-                prepare(h + ROWS_PER_QUANTISE)
             slot = h % ROWS_PER_STORE
             for branch in branch_order:
                 if slot == 0:
@@ -176,6 +185,11 @@ def tile_modelnew_pa_t_kernel(tc, x, w1_words, w1_scales, b1, out_0, out_1, out_
                     nc.gpsimd.tensor_tensor(out=row, in0=row, in1=bias_cols, op=ADD)
                 else:
                     nc.vector.tensor_tensor(out=row, in0=bank[:], in1=bias_cols, op=ADD)
+            if h % ROWS_PER_QUANTISE == 0 and h + ROWS_PER_QUANTISE < H:
+                prepare(h + ROWS_PER_QUANTISE)
+            group = GROUPS_BEFORE_LOOP + h // (B // 2)
+            if RUN * group < H:
+                regroup(nc.scalar.copy, h % (B // 2), group)
             for branch in branch_order:
                 for shift, first, width in branch_pieces(branch):
                     at = first - branch * C
@@ -191,9 +205,9 @@ def tile_modelnew_pa_t_kernel(tc, x, w1_words, w1_scales, b1, out_0, out_1, out_
                     )
 
         by_point = keep.tile([P, C], F32)
-        nc.vector.tensor_copy(out=by_point[:], in_=pooled_sum[:])
+        nc.vector.tensor_tensor(out=by_point[:], in0=pooled_sum[:], in1=bias_pooled[:], op=ADD)
         by_batch = banks.tile([P, C], F32, name="bank")
         nc.tensor.matmul(out=by_batch[:], lhsT=same_batch[:], rhs=by_point[:], start=True, stop=True)
         a_rows = keep.tile([P, C], F32)
-        nc.vector.tensor_tensor(out=a_rows[:], in0=by_batch[:], in1=bias_pooled[:], op=ADD)
+        nc.scalar.copy(out=a_rows[:], in_=by_batch[:])
         nc.sync.dma_start(out=out_3, in_=a_rows[0:B, :])

@@ -180,11 +180,7 @@ def tile_modelnew_pa_t_kernel(tc, x, w1_words, w1_scales, b1, out_0, out_1, out_
                     project(bank[:, at : at + width], shift, h, first, width, True, True)
                 row = rows_out[branch][:, slot, :]
                 bias_cols = bias[:, branch * C : (branch + 1) * C]
-                if branch == 2:
-                    nc.scalar.copy(out=row, in_=bank[:])
-                    nc.gpsimd.tensor_tensor(out=row, in0=row, in1=bias_cols, op=ADD)
-                else:
-                    nc.vector.tensor_tensor(out=row, in0=bank[:], in1=bias_cols, op=ADD)
+                nc.vector.tensor_tensor(out=row, in0=bank[:], in1=bias_cols, op=ADD)
             if h % ROWS_PER_QUANTISE == 0 and h + ROWS_PER_QUANTISE < H:
                 prepare(h + ROWS_PER_QUANTISE)
             group = GROUPS_BEFORE_LOOP + h // (B // 2)

@@ -83,11 +83,9 @@ def tile_modelnew_pa_t_kernel(tc, x, w1_words, w1_scales, b1, out_0, out_1, out_
         nc.vector.memset(h_fold[:], float(H))
         bias_pooled = keep.tile([P, C], F32)
         spread = banks.tile([P, C], F32, name="bank")
-        for branch in range(BRANCHES):
+        for branch in (1, 2):
             cols = slice(branch * C, (branch + 1) * C)
-            nc.tensor.matmul(
-                out=spread[:], lhsT=h_fold[:], rhs=bias_row[:, cols], start=branch == 0, stop=branch == BRANCHES - 1
-            )
+            nc.tensor.matmul(out=spread[:], lhsT=h_fold[:], rhs=bias_row[:, cols], start=branch == 1, stop=branch == 2)
         nc.scalar.copy(out=bias_pooled[:], in_=spread[:])
 
         identity = keep.tile([P, P], F32)
@@ -166,6 +164,8 @@ def tile_modelnew_pa_t_kernel(tc, x, w1_words, w1_scales, b1, out_0, out_1, out_
             )
 
         pooled_sum = pooled.tile([P, C], F32)
+        x1_sum = keep.tile([P, C], F32)
+        nc.gpsimd.memset(x1_sum[:], 0.0)
         branch_order = (2, 0, 1)
         prepare(0)
         rows_out = {}
@@ -181,12 +181,14 @@ def tile_modelnew_pa_t_kernel(tc, x, w1_words, w1_scales, b1, out_0, out_1, out_
                 row = rows_out[branch][:, slot, :]
                 bias_cols = bias[:, branch * C : (branch + 1) * C]
                 nc.vector.tensor_tensor(out=row, in0=bank[:], in1=bias_cols, op=ADD)
+                if branch == 0:
+                    nc.gpsimd.tensor_tensor(out=x1_sum[:], in0=x1_sum[:], in1=row, op=ADD)
             if h % ROWS_PER_QUANTISE == 0 and h + ROWS_PER_QUANTISE < H:
                 prepare(h + ROWS_PER_QUANTISE)
             group = GROUPS_BEFORE_LOOP + h // (B // 2)
             if RUN * group < H:
                 regroup(nc.scalar.copy, h % (B // 2), group)
-            for branch in branch_order:
+            for branch in (2, 1):
                 for shift, first, width in branch_pieces(branch):
                     at = first - branch * C
                     opens = h == 0 and branch == branch_order[0]
@@ -202,6 +204,7 @@ def tile_modelnew_pa_t_kernel(tc, x, w1_words, w1_scales, b1, out_0, out_1, out_
 
         by_point = keep.tile([P, C], F32)
         nc.vector.tensor_tensor(out=by_point[:], in0=pooled_sum[:], in1=bias_pooled[:], op=ADD)
+        nc.vector.tensor_tensor(out=by_point[:], in0=by_point[:], in1=x1_sum[:], op=ADD)
         by_batch = banks.tile([P, C], F32, name="bank")
         nc.tensor.matmul(out=by_batch[:], lhsT=same_batch[:], rhs=by_point[:], start=True, stop=True)
         a_rows = keep.tile([P, C], F32)

@@ -25,7 +25,7 @@ X2_SHIFTS = (H_MINUS, H_PLUS, W_MINUS, W_PLUS)
 
 RUN = 4
 ROWS_PER_QUANTISE = 4
-ROWS_PER_STORE = 2
+ROWS_PER_STORE = 4
 GROUPS_BEFORE_LOOP = 3
 
 
@@ -44,7 +44,7 @@ def tile_modelnew_pa_t_kernel(tc, x, w1_words, w1_scales, b1, out_0, out_1, out_
         ctx.enter_context(tc.manual_schedule())
         keep = ctx.enter_context(tc.tile_pool(name="keep", bufs=1))
         loads = ctx.enter_context(tc.tile_pool(name="loads", bufs=B // 2))
-        results = ctx.enter_context(tc.tile_pool(name="results", bufs=4))
+        results = ctx.enter_context(tc.tile_pool(name="results", bufs=3))
         banks = ctx.enter_context(tc.psum_pool(name="banks", bufs=7))
         pooled = ctx.enter_context(tc.psum_pool(name="pooled", bufs=1))
 
@@ -83,9 +83,11 @@ def tile_modelnew_pa_t_kernel(tc, x, w1_words, w1_scales, b1, out_0, out_1, out_
         nc.vector.memset(h_fold[:], float(H))
         bias_pooled = keep.tile([P, C], F32)
         spread = banks.tile([P, C], F32, name="bank")
-        for branch in (1, 2):
+        for branch in range(BRANCHES):
             cols = slice(branch * C, (branch + 1) * C)
-            nc.tensor.matmul(out=spread[:], lhsT=h_fold[:], rhs=bias_row[:, cols], start=branch == 1, stop=branch == 2)
+            nc.tensor.matmul(
+                out=spread[:], lhsT=h_fold[:], rhs=bias_row[:, cols], start=branch == 0, stop=branch == BRANCHES - 1
+            )
         nc.scalar.copy(out=bias_pooled[:], in_=spread[:])
 
         identity = keep.tile([P, P], F32)
@@ -164,8 +166,6 @@ def tile_modelnew_pa_t_kernel(tc, x, w1_words, w1_scales, b1, out_0, out_1, out_
             )
 
         pooled_sum = pooled.tile([P, C], F32)
-        x1_sum = keep.tile([P, C], F32)
-        nc.gpsimd.memset(x1_sum[:], 0.0)
         branch_order = (2, 0, 1)
         prepare(0)
         rows_out = {}
@@ -180,15 +180,17 @@ def tile_modelnew_pa_t_kernel(tc, x, w1_words, w1_scales, b1, out_0, out_1, out_
                     project(bank[:, at : at + width], shift, h, first, width, True, True)
                 row = rows_out[branch][:, slot, :]
                 bias_cols = bias[:, branch * C : (branch + 1) * C]
-                nc.vector.tensor_tensor(out=row, in0=bank[:], in1=bias_cols, op=ADD)
-                if branch == 0:
-                    nc.gpsimd.tensor_tensor(out=x1_sum[:], in0=x1_sum[:], in1=row, op=ADD)
+                if branch == 2:
+                    nc.scalar.copy(out=row, in_=bank[:])
+                    nc.gpsimd.tensor_tensor(out=row, in0=row, in1=bias_cols, op=ADD)
+                else:
+                    nc.vector.tensor_tensor(out=row, in0=bank[:], in1=bias_cols, op=ADD)
             if h % ROWS_PER_QUANTISE == 0 and h + ROWS_PER_QUANTISE < H:
                 prepare(h + ROWS_PER_QUANTISE)
             group = GROUPS_BEFORE_LOOP + h // (B // 2)
             if RUN * group < H:
                 regroup(nc.scalar.copy, h % (B // 2), group)
-            for branch in (2, 1):
+            for branch in branch_order:
                 for shift, first, width in branch_pieces(branch):
                     at = first - branch * C
                     opens = h == 0 and branch == branch_order[0]
@@ -204,7 +206,6 @@ def tile_modelnew_pa_t_kernel(tc, x, w1_words, w1_scales, b1, out_0, out_1, out_
 
         by_point = keep.tile([P, C], F32)
         nc.vector.tensor_tensor(out=by_point[:], in0=pooled_sum[:], in1=bias_pooled[:], op=ADD)
-        nc.vector.tensor_tensor(out=by_point[:], in0=by_point[:], in1=x1_sum[:], op=ADD)
         by_batch = banks.tile([P, C], F32, name="bank")
         nc.tensor.matmul(out=by_batch[:], lhsT=same_batch[:], rhs=by_point[:], start=True, stop=True)
         a_rows = keep.tile([P, C], F32)

@@ -11,30 +11,26 @@ U8 = mybir.dt.uint8
 FP8X4 = mybir.dt.float8_e4m3fn_x4
 FP4X4 = mybir.dt.float4_e2m1fn_x4
 ADD = mybir.AluOpType.add
+IDENTITY = mybir.ActivationFunctionType.Identity
 
 B, C, W, H = 8, 512, 16, 32
 P = 128
 PACK = 4
+ROWS = 4
+G = H // ROWS
 QUARTER = C // 4
 BRANCHES = 3
 FLOPS = 2 * B * W * H * C * BRANCHES * C
 
 SAME, W_MINUS, W_PLUS, H_MINUS, H_PLUS = 0, 1, 2, 3, 4
-X1_SHIFTS = (W_MINUS, W_PLUS, H_MINUS, H_PLUS)
-X2_SHIFTS = (H_MINUS, H_PLUS, W_MINUS, W_PLUS)
+SHIFTS = (
+    (W_MINUS, W_PLUS, H_MINUS, H_PLUS),
+    (H_MINUS, H_PLUS, W_MINUS, W_PLUS),
+    (SAME, SAME, SAME, SAME),
+)
 
-RUN = 4
-ROWS_PER_QUANTISE = 4
-ROWS_PER_STORE = 4
-GROUPS_BEFORE_LOOP = 3
-
-
-def branch_pieces(branch):
-    if branch == 0:
-        return [(s, q * QUARTER, QUARTER) for q, s in enumerate(X1_SHIFTS)]
-    if branch == 1:
-        return [(s, C + q * QUARTER, QUARTER) for q, s in enumerate(X2_SHIFTS)]
-    return [(SAME, 2 * C, C)]
+ROWS_PER_STORE = 2
+SETS = 2
 
 
 def tile_modelnew_pa_t_kernel(tc, x, w1_words, w1_scales, b1, out_0, out_1, out_2, out_3):
@@ -43,10 +39,10 @@ def tile_modelnew_pa_t_kernel(tc, x, w1_words, w1_scales, b1, out_0, out_1, out_
     with ExitStack() as ctx:
         ctx.enter_context(tc.manual_schedule())
         keep = ctx.enter_context(tc.tile_pool(name="keep", bufs=1))
-        loads = ctx.enter_context(tc.tile_pool(name="loads", bufs=B // 2))
-        results = ctx.enter_context(tc.tile_pool(name="results", bufs=3))
-        banks = ctx.enter_context(tc.psum_pool(name="banks", bufs=7))
-        pooled = ctx.enter_context(tc.psum_pool(name="pooled", bufs=1))
+        loads = ctx.enter_context(tc.tile_pool(name="loads", bufs=B))
+        results = ctx.enter_context(tc.tile_pool(name="results", bufs=4))
+        unread = ctx.enter_context(tc.tile_pool(name="unread", bufs=4))
+        banks = ctx.enter_context(tc.psum_pool(name="banks", bufs=8))
 
         w_words = keep.tile([P, 2 * BRANCHES * C], U8, align_bytes=64)
         w_plane = keep.tile([P, BRANCHES * C], U8, align_bytes=64)
@@ -56,158 +52,174 @@ def tile_modelnew_pa_t_kernel(tc, x, w1_words, w1_scales, b1, out_0, out_1, out_
                 out=w_plane[32 * quadrant : 32 * quadrant + 4, :].bitcast(I32),
                 in_=w1_scales[0, 4 * quadrant : 4 * quadrant + 4, :].bitcast(I32),
             )
-        nc.sync.dma_start(out=w_words[:].bitcast(I32), in_=w1_words[0].bitcast(I32))
-
         bias_row = keep.tile([P, BRANCHES * C], BF16)
         nc.vector.memset(bias_row[:], 0.0)
         nc.sync.dma_start(out=bias_row[0:1, :], in_=b1.rearrange("(o n) -> o n", o=1))
+        nc.sync.dma_start(out=w_words[:].bitcast(I32), in_=w1_words[0].bitcast(I32))
 
         raw = []
-        for pair in range(B // 2):
-            raw_pair = loads.tile([P, 2, PACK * W * H], BF16, name="raw_pair")
-            nc.sync.dma_start(
-                out=raw_pair[:],
-                in_=x[2 * pair : 2 * pair + 2].rearrange("b (p j) w h -> p b (j w h)", j=PACK),
-            )
-            raw.append(raw_pair)
+        for b in range(B):
+            raw_b = loads.tile([P, PACK * W * H], BF16, name="raw_b")
+            nc.sync.dma_start(out=raw_b[:], in_=x[b].rearrange("(p j) w h -> p (j w h)", j=PACK))
+            raw.append(raw_b)
+
+        grouped = []
+        words = []
+        planes = []
+        for s in range(SETS):
+            grouped.append(keep.tile([P, ROWS + 2, P, PACK], BF16, name="grouped%d" % s, align_bytes=64))
+            words.append({})
+            planes.append({})
+            for shift, rows in ((SAME, ROWS + 2), (W_MINUS, ROWS), (W_PLUS, ROWS)):
+                words[s][shift] = keep.tile([P, rows, P], U32, name="words%d_%d" % (s, shift), align_bytes=64)
+                planes[s][shift] = keep.tile([P, rows, P], U8, name="planes%d_%d" % (s, shift), align_bytes=64)
+            nc.vector.memset(planes[s][SAME][:].bitcast(I32), 0)
 
         ones = keep.tile([P, P], BF16)
         nc.vector.memset(ones[:], 1.0)
+        a_by_channel = keep.tile([P, P], F32)
+        nc.vector.memset(a_by_channel[:], 0.0)
+        identity = keep.tile([P, P], F32)
+        make_identity(nc, identity[:])
+
+        def regroup(copy, b, i):
+            by_row = raw[b][:].rearrange("p (j m i) -> p j m i", j=PACK, i=ROWS)
+            copy(out=grouped[b % SETS][:, 1 + i, :, :], in_=by_row[:, :, :, i].rearrange("p j m -> p m j"))
+
+        def move_in_w(tiles, step):
+            same = tiles[SAME][:].bitcast(I32)[:, 1 : 1 + ROWS, :]
+            minus = tiles[W_MINUS][:].bitcast(I32)
+            plus = tiles[W_PLUS][:].bitcast(I32)
+            n = same.shape[2]
+            nc.vector.tensor_copy(out=minus[:, :, step:n], in_=same[:, :, 0 : n - step])
+            nc.vector.tensor_copy(out=minus[:, :, 0:step], in_=same[:, :, 0:step])
+            nc.vector.tensor_copy(out=plus[:, :, 0 : n - step], in_=same[:, :, step:n])
+            nc.vector.tensor_copy(out=plus[:, :, n - step : n], in_=same[:, :, n - step : n])
+
+        def prepare(b):
+            s = b % SETS
+            by_g = grouped[s][:].rearrange("p r (w g) j -> p r w g j", g=G)
+            nc.vector.tensor_copy(out=by_g[:, 0, :, 1:G, :], in_=by_g[:, ROWS, :, 0 : G - 1, :])
+            nc.vector.tensor_copy(out=by_g[:, 0, :, 0, :], in_=by_g[:, 1, :, 0, :])
+            nc.vector.tensor_copy(out=by_g[:, ROWS + 1, :, 0 : G - 1, :], in_=by_g[:, 1, :, 1:G, :])
+            nc.vector.tensor_copy(out=by_g[:, ROWS + 1, :, G - 1, :], in_=by_g[:, ROWS, :, G - 1, :])
+            for rows in (slice(0, ROWS), slice(ROWS, ROWS + 2)):
+                nc.vector.quantize_mx(
+                    out=words[s][SAME][:, rows, :].rearrange("p r m -> p (r m)").bitcast(FP8X4),
+                    scales=planes[s][SAME][:, rows, :].rearrange("p r m -> p (r m)"),
+                    in_=grouped[s][:, rows, :, :].rearrange("p r m j -> p (r m j)"),
+                )
+            move_in_w(words[s], G)
+            move_in_w(planes[s], G // 4)
+
+        def shifted_rows(b, shift, first_row, rows):
+            s = b % SETS
+            if shift in (W_MINUS, W_PLUS):
+                source, at = shift, first_row
+            else:
+                source, at = SAME, first_row + {H_MINUS: 0, SAME: 1, H_PLUS: 2}[shift]
+            return (
+                words[s][source][:, at : at + rows, :].rearrange("p r m -> p (r m)").bitcast(FP8X4),
+                planes[s][source][:, at : at + rows, :].rearrange("p r m -> p (r m)"),
+            )
+
+        def weight_columns(first, width):
+            return (
+                w_words[:, 2 * first : 2 * (first + width)].bitcast(FP4X4),
+                w_plane[:, first : first + width],
+            )
+
+        for i in range(ROWS):
+            regroup(nc.vector.tensor_copy, 0, i)
+        prepare(0)
+
         bias = keep.tile([P, BRANCHES * C], F32)
         for branch in range(BRANCHES):
             cols = slice(branch * C, (branch + 1) * C)
             spread = banks.tile([P, C], F32, name="bank")
             nc.tensor.matmul(out=spread[:], lhsT=ones[:], rhs=bias_row[:, cols], start=True, stop=True)
             nc.scalar.copy(out=bias[:, cols], in_=spread[:])
-        h_fold = keep.tile([P, P], BF16)
-        nc.vector.memset(h_fold[:], float(H))
-        bias_pooled = keep.tile([P, C], F32)
         spread = banks.tile([P, C], F32, name="bank")
         for branch in range(BRANCHES):
             cols = slice(branch * C, (branch + 1) * C)
             nc.tensor.matmul(
-                out=spread[:], lhsT=h_fold[:], rhs=bias_row[:, cols], start=branch == 0, stop=branch == BRANCHES - 1
+                out=spread[:], lhsT=ones[:], rhs=bias_row[:, cols], start=branch == 0, stop=branch == BRANCHES - 1
             )
-        nc.scalar.copy(out=bias_pooled[:], in_=spread[:])
+        bias_sum = keep.tile([P, C], F32)
+        nc.scalar.copy(out=bias_sum[:], in_=spread[:])
+        turned = banks.tile([P, 4, P], F32, name="bank")
+        for q in range(4):
+            nc.tensor.transpose(turned[:, q, :], bias_sum[:, q * QUARTER : (q + 1) * QUARTER], identity[:])
+        bias_by_channel = keep.tile([P, 4], F32)
+        nc.vector.tensor_copy(out=bias_by_channel[:], in_=turned[:, :, 0])
 
-        identity = keep.tile([P, P], F32)
-        make_identity(nc, identity[:])
-        same_batch = keep.tile([P, P], F32)
-        nc.vector.memset(same_batch[:], 0.0)
-        nc.vector.tensor_reduce(
-            out=same_batch[:, 0:B],
-            in_=identity[:].rearrange("p (w b) -> p b w", b=B),
-            axis=mybir.AxisListType.X,
-            op=ADD,
-        )
+        for i in range(ROWS):
+            regroup(nc.scalar.copy, 1, i)
 
-        words = {}
-        planes = {}
-        for shift in (SAME, W_MINUS, W_PLUS):
-            words[shift] = keep.tile([P, H, P], U32, name="words%d" % shift, align_bytes=64)
-            planes[shift] = keep.tile([P, H, P], U8, name="planes%d" % shift, align_bytes=64)
-        nc.vector.memset(planes[SAME][:].bitcast(I32), 0)
-
-        grouped = keep.tile([P, H, W, B * PACK], BF16, align_bytes=64)
-
-        def regroup(copy, pair, group):
-            by_channel = raw[pair][:].rearrange("p b (j w h) -> p (b j) w h", j=PACK, w=W)
-            cols = slice(2 * PACK * pair, 2 * PACK * (pair + 1))
-            rows = slice(RUN * group, RUN * (group + 1))
-            copy(
-                out=grouped[:, rows, :, cols].rearrange("p i w c -> p w c i"),
-                in_=by_channel[:, :, :, rows].rearrange("p c w i -> p w c i"),
-            )
-
-        for pair in range(B // 2):
-            for group in range(GROUPS_BEFORE_LOOP):
-                regroup(nc.vector.tensor_copy, pair, group)
-
-
-        def quantise(first_row):
-            rows = slice(first_row, first_row + ROWS_PER_QUANTISE)
-            nc.vector.quantize_mx(
-                out=words[SAME][:, rows, :].rearrange("p r m -> p (r m)").bitcast(FP8X4),
-                scales=planes[SAME][:, rows, :].rearrange("p r m -> p (r m)"),
-                in_=grouped[:, rows, :, :].rearrange("p r w c -> p (r w c)"),
-            )
-
-        def move_in_w(tiles, rows, step):
-            same = tiles[SAME][:].bitcast(I32)
-            minus = tiles[W_MINUS][:].bitcast(I32)
-            plus = tiles[W_PLUS][:].bitcast(I32)
-            n = same.shape[2]
-            nc.vector.tensor_copy(out=minus[:, rows, step:n], in_=same[:, rows, 0 : n - step])
-            nc.vector.tensor_copy(out=minus[:, rows, 0:step], in_=same[:, rows, 0:step])
-            nc.vector.tensor_copy(out=plus[:, rows, 0 : n - step], in_=same[:, rows, step:n])
-            nc.vector.tensor_copy(out=plus[:, rows, n - step : n], in_=same[:, rows, n - step : n])
-
-        def prepare(first_row):
-            quantise(first_row)
-            rows = slice(first_row, first_row + ROWS_PER_QUANTISE)
-            move_in_w(words, rows, B)
-            move_in_w(planes, rows, B // 4)
-
-        def project(out, shift, h, first, width, start, stop):
-            if shift == H_MINUS:
-                source, row = SAME, max(h - 1, 0)
-            elif shift == H_PLUS:
-                source, row = SAME, min(h + 1, H - 1)
-            else:
-                source, row = shift, h
-            nc.tensor.matmul_mx(
-                out=out,
-                lhsT=words[source][:, row, :].bitcast(FP8X4),
-                lhsT_scale=planes[source][:, row, :],
-                rhs=w_words[:, 2 * first : 2 * (first + width)].bitcast(FP4X4),
-                rhs_scale=w_plane[:, first : first + width],
-                start=start,
-                stop=stop,
-            )
-
-        pooled_sum = pooled.tile([P, C], F32)
-        branch_order = (2, 0, 1)
-        prepare(0)
         rows_out = {}
-        for h in range(H):
-            slot = h % ROWS_PER_STORE
-            for branch in branch_order:
-                if slot == 0:
-                    rows_out[branch] = results.tile([P, ROWS_PER_STORE, C], F32, name="rows%d" % branch)
+        for b in range(B):
+            for i in range(ROWS):
+                slot = i % ROWS_PER_STORE
+                for branch in (2, 0, 1):
+                    if slot == 0:
+                        rows_out[branch] = results.tile([P, ROWS_PER_STORE, C], F32, name="rows%d" % branch)
+                    bank = banks.tile([P, C], F32, name="bank")
+                    width = C if branch == 2 else QUARTER
+                    for at in range(0, C, width):
+                        points, point_scales = shifted_rows(b, SHIFTS[branch][at // QUARTER], i, 1)
+                        columns, column_scales = weight_columns(branch * C + at, width)
+                        nc.tensor.matmul_mx(
+                            out=bank[:, at : at + width],
+                            lhsT=points,
+                            lhsT_scale=point_scales,
+                            rhs=columns,
+                            rhs_scale=column_scales,
+                            start=True,
+                            stop=True,
+                        )
+                    row = rows_out[branch][:, slot, :]
+                    bias_cols = bias[:, branch * C : (branch + 1) * C]
+                    if branch == 2:
+                        nc.scalar.copy(out=row, in_=bank[:])
+                        nc.gpsimd.tensor_tensor(out=row, in0=row, in1=bias_cols, op=ADD)
+                    else:
+                        nc.vector.tensor_tensor(out=row, in0=bank[:], in1=bias_cols, op=ADD)
+                q = i
                 bank = banks.tile([P, C], F32, name="bank")
-                for shift, first, width in branch_pieces(branch):
-                    at = first - branch * C
-                    project(bank[:, at : at + width], shift, h, first, width, True, True)
-                row = rows_out[branch][:, slot, :]
-                bias_cols = bias[:, branch * C : (branch + 1) * C]
-                if branch == 2:
-                    nc.scalar.copy(out=row, in_=bank[:])
-                    nc.gpsimd.tensor_tensor(out=row, in0=row, in1=bias_cols, op=ADD)
-                else:
-                    nc.vector.tensor_tensor(out=row, in0=bank[:], in1=bias_cols, op=ADD)
-            if h % ROWS_PER_QUANTISE == 0 and h + ROWS_PER_QUANTISE < H:
-                prepare(h + ROWS_PER_QUANTISE)
-            group = GROUPS_BEFORE_LOOP + h // (B // 2)
-            if RUN * group < H:
-                regroup(nc.scalar.copy, h % (B // 2), group)
-            for branch in branch_order:
-                for shift, first, width in branch_pieces(branch):
-                    at = first - branch * C
-                    opens = h == 0 and branch == branch_order[0]
-                    closes = h == H - 1 and first + width == 2 * C
-                    project(pooled_sum[:, at : at + width], shift, h, first, width, opens, closes)
-            if slot == ROWS_PER_STORE - 1:
-                first_row = h - slot
-                for branch in branch_order:
-                    nc.sync.dma_start(
-                        out=outs[branch].rearrange("b w h c -> w b (h c)")[:, :, first_row * C : (h + 1) * C],
-                        in_=rows_out[branch][:].rearrange("p r c -> p (r c)"),
+                for branch in range(BRANCHES):
+                    points, point_scales = shifted_rows(b, SHIFTS[branch][q], 0, ROWS)
+                    columns, column_scales = weight_columns(branch * C + q * QUARTER, QUARTER)
+                    nc.tensor.matmul_mx(
+                        out=bank[:],
+                        lhsT=columns,
+                        lhsT_scale=column_scales,
+                        rhs=points,
+                        rhs_scale=point_scales,
+                        start=branch == 0,
+                        stop=branch == BRANCHES - 1,
                     )
+                with_bias = unread.tile([P, C], F32)
+                nc.scalar.activation(
+                    out=with_bias[:],
+                    in_=bank[:],
+                    func=IDENTITY,
+                    bias=bias_by_channel[:, q : q + 1],
+                    accum_out=a_by_channel[:, 4 * b + q : 4 * b + q + 1],
+                )
+                if b + 2 < B:
+                    regroup(nc.scalar.copy, b + 2, i)
+                if i == 0 and b + 1 < B:
+                    prepare(b + 1)
+                if slot == ROWS_PER_STORE - 1:
+                    for branch in (2, 0, 1):
+                        by_partition = outs[branch][b].rearrange("w (g i) c -> (w g) (i c)", i=ROWS)
+                        nc.sync.dma_start(
+                            out=by_partition[:, (i - slot) * C : (i + 1) * C],
+                            in_=rows_out[branch][:].rearrange("p r c -> p (r c)"),
+                        )
 
-        by_point = keep.tile([P, C], F32)
-        nc.vector.tensor_tensor(out=by_point[:], in0=pooled_sum[:], in1=bias_pooled[:], op=ADD)
-        by_batch = banks.tile([P, C], F32, name="bank")
-        nc.tensor.matmul(out=by_batch[:], lhsT=same_batch[:], rhs=by_point[:], start=True, stop=True)
-        a_rows = keep.tile([P, C], F32)
-        nc.scalar.copy(out=a_rows[:], in_=by_batch[:])
-        nc.sync.dma_start(out=out_3, in_=a_rows[0:B, :])
+        turned = banks.tile([P, P], F32, name="bank")
+        nc.tensor.transpose(turned[:], a_by_channel[:], identity[:])
+        a_rows = keep.tile([P, P], F32)
+        nc.scalar.copy(out=a_rows[:], in_=turned[:])
+        nc.sync.dma_start(out=out_3.rearrange("b (q c) -> (b q) c", c=QUARTER), in_=a_rows[0 : 4 * B, :])

@@ -47,6 +47,14 @@ def tile_modelnew_pa_t_kernel(tc, x, w1_words, w1_scales, b1, out_0, out_1, out_
         w_words = keep.tile([P, 2 * BRANCHES * C], U8, align_bytes=64)
         w_plane = keep.tile([P, BRANCHES * C], U8, align_bytes=64)
         nc.vector.memset(w_plane[:].bitcast(I32), 0)
+        raw = []
+        for b in range(B):
+            raw.append(loads.tile([P, PACK * W * H], BF16, name="raw_b"))
+
+        def load(b):
+            nc.sync.dma_start(out=raw[b][:], in_=x[b].rearrange("(p j) w h -> p (j w h)", j=PACK))
+
+        load(0)
         for quadrant in range(4):
             nc.sync.dma_start(
                 out=w_plane[32 * quadrant : 32 * quadrant + 4, :].bitcast(I32),
@@ -57,11 +65,8 @@ def tile_modelnew_pa_t_kernel(tc, x, w1_words, w1_scales, b1, out_0, out_1, out_
         nc.sync.dma_start(out=bias_row[0:1, :], in_=b1.rearrange("(o n) -> o n", o=1))
         nc.sync.dma_start(out=w_words[:].bitcast(I32), in_=w1_words[0].bitcast(I32))
 
-        raw = []
-        for b in range(B):
-            raw_b = loads.tile([P, PACK * W * H], BF16, name="raw_b")
-            nc.sync.dma_start(out=raw_b[:], in_=x[b].rearrange("(p j) w h -> p (j w h)", j=PACK))
-            raw.append(raw_b)
+        for b in range(1, B):
+            load(b)
 
         grouped = []
         words = []
@@ -181,7 +186,13 @@ def tile_modelnew_pa_t_kernel(tc, x, w1_words, w1_scales, b1, out_0, out_1, out_
                     bias_cols = bias[:, branch * C : (branch + 1) * C]
                     if branch == 2:
                         nc.scalar.copy(out=row, in_=bank[:])
-                        nc.gpsimd.tensor_tensor(out=row, in0=row, in1=bias_cols, op=ADD)
+                        if slot == ROWS_PER_STORE - 1:
+                            nc.gpsimd.tensor_tensor(
+                                out=rows_out[branch][:],
+                                in0=rows_out[branch][:],
+                                in1=bias_cols.unsqueeze(1).to_broadcast([P, ROWS_PER_STORE, C]),
+                                op=ADD,
+                            )
                     else:
                         nc.vector.tensor_tensor(out=row, in0=bank[:], in1=bias_cols, op=ADD)
                 q = i

@@ -18,7 +18,8 @@ P = 128
 PACK = 4
 ROWS = 4
 G = H // ROWS
-QUARTER = C // 4
+QUARTERS = 4
+QUARTER = C // QUARTERS
 BRANCHES = 3
 FLOPS = 2 * B * W * H * C * BRANCHES * C
 
@@ -31,6 +32,7 @@ SHIFTS = (
 
 ROWS_PER_STORE = 2
 SETS = 2
+ONES_WIDTH = 32
 
 
 def tile_modelnew_pa_t_kernel(tc, x, w1_words, w1_scales, b1, out_0, out_1, out_2, out_3):
@@ -47,14 +49,6 @@ def tile_modelnew_pa_t_kernel(tc, x, w1_words, w1_scales, b1, out_0, out_1, out_
         w_words = keep.tile([P, 2 * BRANCHES * C], U8, align_bytes=64)
         w_plane = keep.tile([P, BRANCHES * C], U8, align_bytes=64)
         nc.vector.memset(w_plane[:].bitcast(I32), 0)
-        raw = []
-        for b in range(B):
-            raw.append(loads.tile([P, PACK * W * H], BF16, name="raw_b"))
-
-        def load(b):
-            nc.sync.dma_start(out=raw[b][:], in_=x[b].rearrange("(p j) w h -> p (j w h)", j=PACK))
-
-        load(0)
         for quadrant in range(4):
             nc.sync.dma_start(
                 out=w_plane[32 * quadrant : 32 * quadrant + 4, :].bitcast(I32),
@@ -63,10 +57,14 @@ def tile_modelnew_pa_t_kernel(tc, x, w1_words, w1_scales, b1, out_0, out_1, out_
         bias_row = keep.tile([P, BRANCHES * C], BF16)
         nc.vector.memset(bias_row[:], 0.0)
         nc.sync.dma_start(out=bias_row[0:1, :], in_=b1.rearrange("(o n) -> o n", o=1))
-        nc.sync.dma_start(out=w_words[:].bitcast(I32), in_=w1_words[0].bitcast(I32))
 
-        for b in range(1, B):
-            load(b)
+        raw = []
+        for b in range(B):
+            raw_b = loads.tile([P, PACK * W * H], BF16, name="raw_b")
+            nc.sync.dma_start(out=raw_b[:], in_=x[b].rearrange("(p j) w h -> p (j w h)", j=PACK))
+            raw.append(raw_b)
+            if b == 0:
+                nc.sync.dma_start(out=w_words[:].bitcast(I32), in_=w1_words[0].bitcast(I32))
 
         grouped = []
         words = []
@@ -75,9 +73,9 @@ def tile_modelnew_pa_t_kernel(tc, x, w1_words, w1_scales, b1, out_0, out_1, out_
             grouped.append(keep.tile([P, ROWS + 2, P, PACK], BF16, name="grouped%d" % s, align_bytes=64))
             words.append({})
             planes.append({})
-            for shift, rows in ((SAME, ROWS + 2), (W_MINUS, ROWS), (W_PLUS, ROWS)):
-                words[s][shift] = keep.tile([P, rows, P], U32, name="words%d_%d" % (s, shift), align_bytes=64)
-                planes[s][shift] = keep.tile([P, rows, P], U8, name="planes%d_%d" % (s, shift), align_bytes=64)
+            for shift, n_rows in ((SAME, ROWS + 2), (W_MINUS, ROWS), (W_PLUS, ROWS)):
+                words[s][shift] = keep.tile([P, n_rows, P], U32, name="words%d_%d" % (s, shift), align_bytes=64)
+                planes[s][shift] = keep.tile([P, n_rows, P], U8, name="planes%d_%d" % (s, shift), align_bytes=64)
             nc.vector.memset(planes[s][SAME][:].bitcast(I32), 0)
 
         ones = keep.tile([P, P], BF16)
@@ -101,31 +99,36 @@ def tile_modelnew_pa_t_kernel(tc, x, w1_words, w1_scales, b1, out_0, out_1, out_
             nc.vector.tensor_copy(out=plus[:, :, 0 : n - step], in_=same[:, :, step:n])
             nc.vector.tensor_copy(out=plus[:, :, n - step : n], in_=same[:, :, n - step : n])
 
+        def quantise(s, first, n_rows):
+            part = slice(first, first + n_rows)
+            nc.vector.quantize_mx(
+                out=words[s][SAME][:, part, :].rearrange("p r m -> p (r m)").bitcast(FP8X4),
+                scales=planes[s][SAME][:, part, :].rearrange("p r m -> p (r m)"),
+                in_=grouped[s][:, part, :, :].rearrange("p r m j -> p (r m j)"),
+            )
+
         def prepare(b):
             s = b % SETS
+            quantise(s, 1, ROWS)
             by_g = grouped[s][:].rearrange("p r (w g) j -> p r w g j", g=G)
             nc.vector.tensor_copy(out=by_g[:, 0, :, 1:G, :], in_=by_g[:, ROWS, :, 0 : G - 1, :])
             nc.vector.tensor_copy(out=by_g[:, 0, :, 0, :], in_=by_g[:, 1, :, 0, :])
             nc.vector.tensor_copy(out=by_g[:, ROWS + 1, :, 0 : G - 1, :], in_=by_g[:, 1, :, 1:G, :])
             nc.vector.tensor_copy(out=by_g[:, ROWS + 1, :, G - 1, :], in_=by_g[:, ROWS, :, G - 1, :])
-            for rows in (slice(0, ROWS), slice(ROWS, ROWS + 2)):
-                nc.vector.quantize_mx(
-                    out=words[s][SAME][:, rows, :].rearrange("p r m -> p (r m)").bitcast(FP8X4),
-                    scales=planes[s][SAME][:, rows, :].rearrange("p r m -> p (r m)"),
-                    in_=grouped[s][:, rows, :, :].rearrange("p r m j -> p (r m j)"),
-                )
             move_in_w(words[s], G)
+            quantise(s, 0, 1)
+            quantise(s, ROWS + 1, 1)
             move_in_w(planes[s], G // 4)
 
-        def shifted_rows(b, shift, first_row, rows):
+        def shifted_rows(b, shift, i, n_rows):
             s = b % SETS
             if shift in (W_MINUS, W_PLUS):
-                source, at = shift, first_row
+                source, first = shift, i
             else:
-                source, at = SAME, first_row + {H_MINUS: 0, SAME: 1, H_PLUS: 2}[shift]
+                source, first = SAME, i + {H_MINUS: 0, SAME: 1, H_PLUS: 2}[shift]
             return (
-                words[s][source][:, at : at + rows, :].rearrange("p r m -> p (r m)").bitcast(FP8X4),
-                planes[s][source][:, at : at + rows, :].rearrange("p r m -> p (r m)"),
+                words[s][source][:, first : first + n_rows, :].rearrange("p r m -> p (r m)").bitcast(FP8X4),
+                planes[s][source][:, first : first + n_rows, :].rearrange("p r m -> p (r m)"),
             )
 
         def weight_columns(first, width):
@@ -144,19 +147,19 @@ def tile_modelnew_pa_t_kernel(tc, x, w1_words, w1_scales, b1, out_0, out_1, out_
             spread = banks.tile([P, C], F32, name="bank")
             nc.tensor.matmul(out=spread[:], lhsT=ones[:], rhs=bias_row[:, cols], start=True, stop=True)
             nc.scalar.copy(out=bias[:, cols], in_=spread[:])
-        spread = banks.tile([P, C], F32, name="bank")
-        for branch in range(BRANCHES):
-            cols = slice(branch * C, (branch + 1) * C)
-            nc.tensor.matmul(
-                out=spread[:], lhsT=ones[:], rhs=bias_row[:, cols], start=branch == 0, stop=branch == BRANCHES - 1
-            )
-        bias_sum = keep.tile([P, C], F32)
-        nc.scalar.copy(out=bias_sum[:], in_=spread[:])
-        turned = banks.tile([P, 4, P], F32, name="bank")
-        for q in range(4):
-            nc.tensor.transpose(turned[:, q, :], bias_sum[:, q * QUARTER : (q + 1) * QUARTER], identity[:])
-        bias_by_channel = keep.tile([P, 4], F32)
-        nc.vector.tensor_copy(out=bias_by_channel[:], in_=turned[:, :, 0])
+        bias_turned = banks.tile([P, QUARTERS, ONES_WIDTH], F32, name="bank")
+        for q in range(QUARTERS):
+            for branch in range(BRANCHES):
+                first = branch * C + q * QUARTER
+                nc.tensor.matmul(
+                    out=bias_turned[:, q, :],
+                    lhsT=bias_row[:, first : first + QUARTER],
+                    rhs=ones[:, 0:ONES_WIDTH],
+                    start=branch == 0,
+                    stop=branch == BRANCHES - 1,
+                )
+        bias_by_channel = keep.tile([P, QUARTERS], F32)
+        nc.scalar.copy(out=bias_by_channel[:], in_=bias_turned[:, :, 0])
 
         for i in range(ROWS):
             regroup(nc.scalar.copy, 1, i)
@@ -182,19 +185,13 @@ def tile_modelnew_pa_t_kernel(tc, x, w1_words, w1_scales, b1, out_0, out_1, out_
                             start=True,
                             stop=True,
                         )
-                    row = rows_out[branch][:, slot, :]
+                    out_row = rows_out[branch][:, slot, :]
                     bias_cols = bias[:, branch * C : (branch + 1) * C]
                     if branch == 2:
-                        nc.scalar.copy(out=row, in_=bank[:])
-                        if slot == ROWS_PER_STORE - 1:
-                            nc.gpsimd.tensor_tensor(
-                                out=rows_out[branch][:],
-                                in0=rows_out[branch][:],
-                                in1=bias_cols.unsqueeze(1).to_broadcast([P, ROWS_PER_STORE, C]),
-                                op=ADD,
-                            )
+                        nc.scalar.copy(out=out_row, in_=bank[:])
+                        nc.gpsimd.tensor_tensor(out=out_row, in0=out_row, in1=bias_cols, op=ADD)
                     else:
-                        nc.vector.tensor_tensor(out=row, in0=bank[:], in1=bias_cols, op=ADD)
+                        nc.vector.tensor_tensor(out=out_row, in0=bank[:], in1=bias_cols, op=ADD)
                 q = i
                 bank = banks.tile([P, C], F32, name="bank")
                 for branch in range(BRANCHES):
@@ -215,7 +212,7 @@ def tile_modelnew_pa_t_kernel(tc, x, w1_words, w1_scales, b1, out_0, out_1, out_
                     in_=bank[:],
                     func=IDENTITY,
                     bias=bias_by_channel[:, q : q + 1],
-                    accum_out=a_by_channel[:, 4 * b + q : 4 * b + q + 1],
+                    accum_out=a_by_channel[:, QUARTERS * b + q : QUARTERS * b + q + 1],
                 )
                 if b + 2 < B:
                     regroup(nc.scalar.copy, b + 2, i)
@@ -229,8 +226,8 @@ def tile_modelnew_pa_t_kernel(tc, x, w1_words, w1_scales, b1, out_0, out_1, out_
                             in_=rows_out[branch][:].rearrange("p r c -> p (r c)"),
                         )
 
-        turned = banks.tile([P, P], F32, name="bank")
-        nc.tensor.transpose(turned[:], a_by_channel[:], identity[:])
+        a_turned = banks.tile([P, P], F32, name="bank")
+        nc.tensor.transpose(a_turned[:], a_by_channel[:], identity[:])
         a_rows = keep.tile([P, P], F32)
-        nc.scalar.copy(out=a_rows[:], in_=turned[:])
-        nc.sync.dma_start(out=out_3.rearrange("b (q c) -> (b q) c", c=QUARTER), in_=a_rows[0 : 4 * B, :])
+        nc.scalar.copy(out=a_rows[:], in_=a_turned[:])
+        nc.sync.dma_start(out=out_3.rearrange("b (q c) -> (b q) c", c=QUARTER), in_=a_rows[0 : QUARTERS * B, :])

@@ -89,7 +89,7 @@ def tile_modelnew_pa_t_kernel(tc, x, w1_words, w1_scales, b1, out_0, out_1, out_
             by_row = raw[b][:].rearrange("p (j m i) -> p j m i", j=PACK, i=ROWS)
             copy(out=grouped[b % SETS][:, 1 + i, :, :], in_=by_row[:, :, :, i].rearrange("p j m -> p m j"))
 
-        def move_in_w(tiles, step):
+        def move_in_w(tiles, step, last_copy):
             same = tiles[SAME][:].bitcast(I32)[:, 1 : 1 + ROWS, :]
             minus = tiles[W_MINUS][:].bitcast(I32)
             plus = tiles[W_PLUS][:].bitcast(I32)
@@ -97,7 +97,10 @@ def tile_modelnew_pa_t_kernel(tc, x, w1_words, w1_scales, b1, out_0, out_1, out_
             nc.vector.tensor_copy(out=minus[:, :, step:n], in_=same[:, :, 0 : n - step])
             nc.vector.tensor_copy(out=minus[:, :, 0:step], in_=same[:, :, 0:step])
             nc.vector.tensor_copy(out=plus[:, :, 0 : n - step], in_=same[:, :, step:n])
-            nc.vector.tensor_copy(out=plus[:, :, n - step : n], in_=same[:, :, n - step : n])
+            if last_copy is None:
+                nc.vector.tensor_copy(out=plus[:, :, n - step : n], in_=same[:, :, n - step : n])
+            else:
+                last_copy(out=plus[:, :, n - step : n], in_=plus[:, :, n - 2 * step : n - step])
 
         def quantise(s, first, n_rows):
             part = slice(first, first + n_rows)
@@ -107,7 +110,7 @@ def tile_modelnew_pa_t_kernel(tc, x, w1_words, w1_scales, b1, out_0, out_1, out_
                 in_=grouped[s][:, part, :, :].rearrange("p r m j -> p (r m j)"),
             )
 
-        def prepare(b):
+        def prepare(b, last_copy):
             s = b % SETS
             quantise(s, 1, ROWS)
             by_g = grouped[s][:].rearrange("p r (w g) j -> p r w g j", g=G)
@@ -115,10 +118,10 @@ def tile_modelnew_pa_t_kernel(tc, x, w1_words, w1_scales, b1, out_0, out_1, out_
             nc.vector.tensor_copy(out=by_g[:, 0, :, 0, :], in_=by_g[:, 1, :, 0, :])
             nc.vector.tensor_copy(out=by_g[:, ROWS + 1, :, 0 : G - 1, :], in_=by_g[:, 1, :, 1:G, :])
             nc.vector.tensor_copy(out=by_g[:, ROWS + 1, :, G - 1, :], in_=by_g[:, ROWS, :, G - 1, :])
-            move_in_w(words[s], G)
+            move_in_w(words[s], G, None)
             quantise(s, 0, 1)
             quantise(s, ROWS + 1, 1)
-            move_in_w(planes[s], G // 4)
+            move_in_w(planes[s], G // 4, last_copy)
 
         def shifted_rows(b, shift, i, n_rows):
             s = b % SETS
@@ -139,7 +142,7 @@ def tile_modelnew_pa_t_kernel(tc, x, w1_words, w1_scales, b1, out_0, out_1, out_
 
         for i in range(ROWS):
             regroup(nc.vector.tensor_copy, 0, i)
-        prepare(0)
+        prepare(0, None)
 
         bias = keep.tile([P, BRANCHES * C], F32)
         for branch in range(BRANCHES):
@@ -217,9 +220,9 @@ def tile_modelnew_pa_t_kernel(tc, x, w1_words, w1_scales, b1, out_0, out_1, out_
                 if b + 2 < B:
                     regroup(nc.scalar.copy, b + 2, i)
                 if i == 0 and b + 1 < B:
-                    prepare(b + 1)
+                    prepare(b + 1, nc.gpsimd.tensor_copy)
                 if slot == ROWS_PER_STORE - 1:
-                    for branch in (2, 0, 1):
+                    for branch in (0, 1, 2):
                         by_partition = outs[branch][b].rearrange("w (g i) c -> (w g) (i c)", i=ROWS)
                         nc.sync.dma_start(
                             out=by_partition[:, (i - slot) * C : (i + 1) * C],

@@ -55,7 +55,7 @@ def tile_modelnew_pa_t_kernel(tc, x, w1_words, w1_scales, b1, out_0, out_1, out_
                 in_=w1_scales[0, 4 * quadrant : 4 * quadrant + 4, :].bitcast(I32),
             )
         bias_row = keep.tile([P, BRANCHES * C], BF16)
-        nc.vector.memset(bias_row[:], 0.0)
+        nc.vector.memset(bias_row[:].bitcast(I32), 0)
         nc.sync.dma_start(out=bias_row[0:1, :], in_=b1.rearrange("(o n) -> o n", o=1))
 
         raw = []
@@ -190,7 +190,7 @@ def tile_modelnew_pa_t_kernel(tc, x, w1_words, w1_scales, b1, out_0, out_1, out_
                         )
                     out_row = rows_out[branch][:, slot, :]
                     bias_cols = bias[:, branch * C : (branch + 1) * C]
-                    if branch == 2:
+                    if branch == 2 and i != (ROWS - 1 if b == B - 1 else 0):
                         nc.scalar.copy(out=out_row, in_=bank[:])
                         nc.gpsimd.tensor_tensor(out=out_row, in0=out_row, in1=bias_cols, op=ADD)
                     else:

@@ -20,6 +20,7 @@ ROWS = 4
 G = H // ROWS
 QUARTERS = 4
 QUARTER = C // QUARTERS
+PAIR = 2 * QUARTER
 BRANCHES = 3
 FLOPS = 2 * B * W * H * C * BRANCHES * C
 
@@ -58,6 +59,18 @@ def tile_modelnew_pa_t_kernel(tc, x, w1_words, w1_scales, b1, out_0, out_1, out_
         nc.vector.memset(bias_row[:].bitcast(I32), 0)
         nc.sync.dma_start(out=bias_row[0:1, :], in_=b1.rearrange("(o n) -> o n", o=1))
 
+        pair_words = keep.tile([P, 2 * 2 * C], U8, align_bytes=64)
+        pair_plane = keep.tile([P, 2 * C], U8, align_bytes=64)
+
+        def paired(dst, src, unit):
+            to = dst.rearrange("p (s two c) -> p s two c", two=2, c=unit)
+            quarters = src.rearrange("p (k c) -> p k c", c=unit)
+            return (
+                (to[:, :, 0, :], quarters[:, 0:4, :]),
+                (to[:, 0:2, 1, :], quarters[:, 6:8, :]),
+                (to[:, 2:4, 1, :], quarters[:, 4:6, :]),
+            )
+
         raw = []
         for b in range(B):
             raw_b = loads.tile([P, PACK * W * H], BF16, name="raw_b")
@@ -65,6 +78,8 @@ def tile_modelnew_pa_t_kernel(tc, x, w1_words, w1_scales, b1, out_0, out_1, out_
             raw.append(raw_b)
             if b == 0:
                 nc.sync.dma_start(out=w_words[:].bitcast(I32), in_=w1_words[0].bitcast(I32))
+                for to, quarters in paired(pair_words[:].bitcast(I32), w1_words[0].bitcast(I32)[:, 0:C], QUARTER // 2):
+                    nc.sync.dma_start(out=to, in_=quarters)
 
         grouped = []
         words = []
@@ -140,6 +155,9 @@ def tile_modelnew_pa_t_kernel(tc, x, w1_words, w1_scales, b1, out_0, out_1, out_
                 w_plane[:, first : first + width],
             )
 
+        for to, quarters in paired(pair_plane[:].bitcast(I32), w_plane[:].bitcast(I32)[:, 0 : C // 2], QUARTER // 4):
+            nc.vector.tensor_copy(out=to, in_=quarters)
+
         for i in range(ROWS):
             regroup(nc.vector.tensor_copy, 0, i)
         prepare(0, None)
@@ -167,34 +185,59 @@ def tile_modelnew_pa_t_kernel(tc, x, w1_words, w1_scales, b1, out_0, out_1, out_
         for i in range(ROWS):
             regroup(nc.scalar.copy, 1, i)
 
-        rows_out = {}
         for b in range(B):
             for i in range(ROWS):
                 slot = i % ROWS_PER_STORE
-                for branch in (2, 0, 1):
-                    if slot == 0:
-                        rows_out[branch] = results.tile([P, ROWS_PER_STORE, C], F32, name="rows%d" % branch)
+                if slot == 0:
+                    rows_x3 = results.tile([P, ROWS_PER_STORE, C], F32, name="rows_x3")
+                    rows_x12 = results.tile([P, 3 * ROWS_PER_STORE * C], F32, name="rows_x12")
+                bank = banks.tile([P, C], F32, name="bank")
+                points, point_scales = shifted_rows(b, SAME, i, 1)
+                columns, column_scales = weight_columns(2 * C, C)
+                nc.tensor.matmul_mx(
+                    out=bank[:],
+                    lhsT=points,
+                    lhsT_scale=point_scales,
+                    rhs=columns,
+                    rhs_scale=column_scales,
+                    start=True,
+                    stop=True,
+                )
+                out_row = rows_x3[:, slot, :]
+                bias_cols = bias[:, 2 * C : 3 * C]
+                if i != (ROWS - 1 if b == B - 1 else 0):
+                    nc.scalar.copy(out=out_row, in_=bank[:])
+                    nc.gpsimd.tensor_tensor(out=out_row, in0=out_row, in1=bias_cols, op=ADD)
+                else:
+                    nc.vector.tensor_tensor(out=out_row, in0=bank[:], in1=bias_cols, op=ADD)
+                for kind, shifts in enumerate(((W_MINUS, W_PLUS), (H_MINUS, H_PLUS))):
                     bank = banks.tile([P, C], F32, name="bank")
-                    width = C if branch == 2 else QUARTER
-                    for at in range(0, C, width):
-                        points, point_scales = shifted_rows(b, SHIFTS[branch][at // QUARTER], i, 1)
-                        columns, column_scales = weight_columns(branch * C + at, width)
+                    for s, shift in enumerate(shifts):
+                        points, point_scales = shifted_rows(b, shift, i, 1)
+                        first = (2 * kind + s) * PAIR
                         nc.tensor.matmul_mx(
-                            out=bank[:, at : at + width],
+                            out=bank[:, s * PAIR : (s + 1) * PAIR],
                             lhsT=points,
                             lhsT_scale=point_scales,
-                            rhs=columns,
-                            rhs_scale=column_scales,
+                            rhs=pair_words[:, 2 * first : 2 * (first + PAIR)].bitcast(FP4X4),
+                            rhs_scale=pair_plane[:, first : first + PAIR],
                             start=True,
                             stop=True,
                         )
-                    out_row = rows_out[branch][:, slot, :]
-                    bias_cols = bias[:, branch * C : (branch + 1) * C]
-                    if branch == 2 and i != (ROWS - 1 if b == B - 1 else 0):
-                        nc.scalar.copy(out=out_row, in_=bank[:])
-                        nc.gpsimd.tensor_tensor(out=out_row, in0=out_row, in1=bias_cols, op=ADD)
+                    one_branch = ROWS_PER_STORE * C
+                    if kind == 0:
+                        at, step = slot * C, one_branch + PAIR
+                        bias_view = bias[:, 0 : 3 * C].rearrange("p (br x) -> p br x", br=2)[:, :, 0:PAIR]
                     else:
-                        nc.vector.tensor_tensor(out=out_row, in0=bank[:], in1=bias_cols, op=ADD)
+                        at, step = slot * C + PAIR, one_branch - PAIR
+                        bias_view = bias[:, PAIR : 3 * PAIR].rearrange("p (br x) -> p br x", br=2)
+                    out_view = rows_x12[:, at : at + 2 * step].rearrange("p (br x) -> p br x", br=2)[:, :, 0:PAIR]
+                    nc.vector.tensor_tensor(
+                        out=out_view.rearrange("p br (s c) -> p br s c", c=QUARTER),
+                        in0=bank[:].rearrange("p (s br c) -> p br s c", s=2, br=2),
+                        in1=bias_view.rearrange("p br (s c) -> p br s c", c=QUARTER),
+                        op=ADD,
+                    )
                 q = i
                 bank = banks.tile([P, C], F32, name="bank")
                 for branch in range(BRANCHES):
@@ -222,12 +265,14 @@ def tile_modelnew_pa_t_kernel(tc, x, w1_words, w1_scales, b1, out_0, out_1, out_
                 if i == 0 and b + 1 < B:
                     prepare(b + 1, nc.gpsimd.tensor_copy)
                 if slot == ROWS_PER_STORE - 1:
-                    for branch in (0, 1, 2):
+                    one_branch = ROWS_PER_STORE * C
+                    for branch, rows in (
+                        (0, rows_x12[:, 0:one_branch]),
+                        (1, rows_x12[:, one_branch : 2 * one_branch]),
+                        (2, rows_x3[:].rearrange("p r c -> p (r c)")),
+                    ):
                         by_partition = outs[branch][b].rearrange("w (g i) c -> (w g) (i c)", i=ROWS)
-                        nc.sync.dma_start(
-                            out=by_partition[:, (i - slot) * C : (i + 1) * C],
-                            in_=rows_out[branch][:].rearrange("p r c -> p (r c)"),
-                        )
+                        nc.sync.dma_start(out=by_partition[:, (i - slot) * C : (i + 1) * C], in_=rows)
 
         a_turned = banks.tile([P, P], F32, name="bank")
         nc.tensor.transpose(a_turned[:], a_by_channel[:], identity[:])

@@ -104,6 +104,14 @@ def tile_modelnew_pa_t_kernel(tc, x, w1_words, w1_scales, b1, out_0, out_1, out_
             by_row = raw[b][:].rearrange("p (j m i) -> p j m i", j=PACK, i=ROWS)
             copy(out=grouped[b % SETS][:, 1 + i, :, :], in_=by_row[:, :, :, i].rearrange("p j m -> p m j"))
 
+        def regroup_columns(b, k):
+            part = slice(k * P // ROWS, (k + 1) * P // ROWS)
+            by_column = raw[b][:].rearrange("p (j m i) -> p j m i", j=PACK, i=ROWS)
+            nc.scalar.copy(
+                out=grouped[b % SETS][:, 1 : 1 + ROWS, part, :].rearrange("p r m j -> p m j r"),
+                in_=by_column[:, :, part, :].rearrange("p j m i -> p m j i"),
+            )
+
         def move_in_w(tiles, step, last_copy):
             same = tiles[SAME][:].bitcast(I32)[:, 1 : 1 + ROWS, :]
             minus = tiles[W_MINUS][:].bitcast(I32)
@@ -183,7 +191,7 @@ def tile_modelnew_pa_t_kernel(tc, x, w1_words, w1_scales, b1, out_0, out_1, out_
         nc.scalar.copy(out=bias_by_channel[:], in_=bias_turned[:, :, 0])
 
         for i in range(ROWS):
-            regroup(nc.scalar.copy, 1, i)
+            regroup_columns(1, i)
 
         for b in range(B):
             for i in range(ROWS):
@@ -261,7 +269,7 @@ def tile_modelnew_pa_t_kernel(tc, x, w1_words, w1_scales, b1, out_0, out_1, out_
                     accum_out=a_by_channel[:, QUARTERS * b + q : QUARTERS * b + q + 1],
                 )
                 if b + 2 < B:
-                    regroup(nc.scalar.copy, b + 2, i)
+                    regroup_columns(b + 2, i)
                 if i == 0 and b + 1 < B:
                     prepare(b + 1, nc.gpsimd.tensor_copy)
                 if slot == ROWS_PER_STORE - 1:

@@ -193,11 +193,16 @@ def tile_modelnew_pa_t_kernel(tc, x, w1_words, w1_scales, b1, out_0, out_1, out_
         for i in range(ROWS):
             regroup_columns(1, i)
 
+        def store(branch, b, columns, rows):
+            by_partition = outs[branch][b].rearrange("w (g i) c -> (w g) (i c)", i=ROWS)
+            nc.sync.dma_start(out=by_partition[:, columns], in_=rows)
+
         for b in range(B):
             for i in range(ROWS):
                 slot = i % ROWS_PER_STORE
+                if i == 0:
+                    rows_x3 = results.tile([P, ROWS, C], F32, name="rows_x3", bufs=3)
                 if slot == 0:
-                    rows_x3 = results.tile([P, ROWS_PER_STORE, C], F32, name="rows_x3")
                     rows_x12 = results.tile([P, 3 * ROWS_PER_STORE * C], F32, name="rows_x12")
                 bank = banks.tile([P, C], F32, name="bank")
                 points, point_scales = shifted_rows(b, SAME, i, 1)
@@ -211,7 +216,7 @@ def tile_modelnew_pa_t_kernel(tc, x, w1_words, w1_scales, b1, out_0, out_1, out_
                     start=True,
                     stop=True,
                 )
-                out_row = rows_x3[:, slot, :]
+                out_row = rows_x3[:, i, :]
                 bias_cols = bias[:, 2 * C : 3 * C]
                 if i != (ROWS - 1 if b == B - 1 else 0):
                     nc.scalar.copy(out=out_row, in_=bank[:])
@@ -274,13 +279,14 @@ def tile_modelnew_pa_t_kernel(tc, x, w1_words, w1_scales, b1, out_0, out_1, out_
                     prepare(b + 1, nc.gpsimd.tensor_copy)
                 if slot == ROWS_PER_STORE - 1:
                     one_branch = ROWS_PER_STORE * C
-                    for branch, rows in (
-                        (0, rows_x12[:, 0:one_branch]),
-                        (1, rows_x12[:, one_branch : 2 * one_branch]),
-                        (2, rows_x3[:].rearrange("p r c -> p (r c)")),
-                    ):
-                        by_partition = outs[branch][b].rearrange("w (g i) c -> (w g) (i c)", i=ROWS)
-                        nc.sync.dma_start(out=by_partition[:, (i - slot) * C : (i + 1) * C], in_=rows)
+                    halves = slice((i - slot) * C, (i + 1) * C)
+                    store(0, b, halves, rows_x12[:, 0:one_branch])
+                    store(1, b, halves, rows_x12[:, one_branch : 2 * one_branch])
+                    x3 = rows_x3[:].rearrange("p r c -> p (r c)")
+                    if b in (0, B - 1):
+                        store(2, b, halves, x3[:, halves])
+                    elif i == ROWS - 1:
+                        store(2, b, slice(0, ROWS * C), x3)
 
         a_turned = banks.tile([P, P], F32, name="bank")
         nc.tensor.transpose(a_turned[:], a_by_channel[:], identity[:])

@@ -47,7 +47,7 @@ def tile_modelnew_pa_t_kernel(tc, x, w1_words, w1_scales, b1, out_0, out_1, out_
         unread = ctx.enter_context(tc.tile_pool(name="unread", bufs=4))
         banks = ctx.enter_context(tc.psum_pool(name="banks", bufs=8))
 
-        w_words = keep.tile([P, 2 * BRANCHES * C], U8, align_bytes=64)
+        x3_words = keep.tile([P, 2 * C], U8, align_bytes=64)
         w_plane = keep.tile([P, BRANCHES * C], U8, align_bytes=64)
         nc.vector.memset(w_plane[:].bitcast(I32), 0)
         for quadrant in range(4):
@@ -76,8 +76,8 @@ def tile_modelnew_pa_t_kernel(tc, x, w1_words, w1_scales, b1, out_0, out_1, out_
             raw_b = loads.tile([P, PACK * W * H], BF16, name="raw_b")
             nc.sync.dma_start(out=raw_b[:], in_=x[b].rearrange("(p j) w h -> p (j w h)", j=PACK))
             raw.append(raw_b)
-            if b == 0:
-                nc.sync.dma_start(out=w_words[:].bitcast(I32), in_=w1_words[0].bitcast(I32))
+            if b == 1:
+                nc.sync.dma_start(out=x3_words[:].bitcast(I32), in_=w1_words[0].bitcast(I32)[:, C : C + C // 2])
                 for to, quarters in paired(pair_words[:].bitcast(I32), w1_words[0].bitcast(I32)[:, 0:C], QUARTER // 2):
                     nc.sync.dma_start(out=to, in_=quarters)
 
@@ -157,17 +157,19 @@ def tile_modelnew_pa_t_kernel(tc, x, w1_words, w1_scales, b1, out_0, out_1, out_
                 planes[s][source][:, first : first + n_rows, :].rearrange("p r m -> p (r m)"),
             )
 
-        def weight_columns(first, width):
-            return (
-                w_words[:, 2 * first : 2 * (first + width)].bitcast(FP4X4),
-                w_plane[:, first : first + width],
-            )
+        def weight_quarter(branch, q):
+            if branch == BRANCHES - 1:
+                source, at = x3_words, q * QUARTER
+            else:
+                source, at = pair_words, (2 * q if branch == 0 else 2 * ((q + 2) % QUARTERS) + 1) * QUARTER
+            first = branch * C + q * QUARTER
+            return source[:, 2 * at : 2 * (at + QUARTER)].bitcast(FP4X4), w_plane[:, first : first + QUARTER]
 
         for to, quarters in paired(pair_plane[:].bitcast(I32), w_plane[:].bitcast(I32)[:, 0 : C // 2], QUARTER // 4):
             nc.vector.tensor_copy(out=to, in_=quarters)
 
         for i in range(ROWS):
-            regroup(nc.vector.tensor_copy, 0, i)
+            regroup(nc.vector.tensor_copy if i < ROWS - 1 else nc.scalar.copy, 0, i)
         prepare(0, None)
 
         bias = keep.tile([P, BRANCHES * C], F32)
@@ -206,13 +208,12 @@ def tile_modelnew_pa_t_kernel(tc, x, w1_words, w1_scales, b1, out_0, out_1, out_
                     rows_x12 = results.tile([P, 3 * ROWS_PER_STORE * C], F32, name="rows_x12")
                 bank = banks.tile([P, C], F32, name="bank")
                 points, point_scales = shifted_rows(b, SAME, i, 1)
-                columns, column_scales = weight_columns(2 * C, C)
                 nc.tensor.matmul_mx(
                     out=bank[:],
                     lhsT=points,
                     lhsT_scale=point_scales,
-                    rhs=columns,
-                    rhs_scale=column_scales,
+                    rhs=x3_words[:].bitcast(FP4X4),
+                    rhs_scale=w_plane[:, 2 * C : 3 * C],
                     start=True,
                     stop=True,
                 )
@@ -255,7 +256,7 @@ def tile_modelnew_pa_t_kernel(tc, x, w1_words, w1_scales, b1, out_0, out_1, out_
                 bank = banks.tile([P, C], F32, name="bank")
                 for branch in range(BRANCHES):
                     points, point_scales = shifted_rows(b, SHIFTS[branch][q], 0, ROWS)
-                    columns, column_scales = weight_columns(branch * C + q * QUARTER, QUARTER)
+                    columns, column_scales = weight_quarter(branch, q)
                     nc.tensor.matmul_mx(
                         out=bank[:],
                         lhsT=columns,

@@ -49,12 +49,20 @@ def tile_modelnew_pa_t_kernel(tc, x, w1_words, w1_scales, b1, out_0, out_1, out_
 
         x3_words = keep.tile([P, 2 * C], U8, align_bytes=64)
         w_plane = keep.tile([P, BRANCHES * C], U8, align_bytes=64)
-        nc.vector.memset(w_plane[:].bitcast(I32), 0)
+        nc.gpsimd.memset(w_plane[:].bitcast(I32), 0)
         for quadrant in range(4):
             nc.sync.dma_start(
                 out=w_plane[32 * quadrant : 32 * quadrant + 4, :].bitcast(I32),
                 in_=w1_scales[0, 4 * quadrant : 4 * quadrant + 4, :].bitcast(I32),
             )
+        raw = []
+
+        def load(b):
+            raw_b = loads.tile([P, PACK * W * H], BF16, name="raw_b")
+            nc.sync.dma_start(out=raw_b[:], in_=x[b].rearrange("(p j) w h -> p (j w h)", j=PACK))
+            raw.append(raw_b)
+
+        load(0)
         bias_row = keep.tile([P, BRANCHES * C], BF16)
         nc.vector.memset(bias_row[:].bitcast(I32), 0)
         nc.sync.dma_start(out=bias_row[0:1, :], in_=b1.rearrange("(o n) -> o n", o=1))
@@ -71,15 +79,12 @@ def tile_modelnew_pa_t_kernel(tc, x, w1_words, w1_scales, b1, out_0, out_1, out_
                 (to[:, 2:4, 1, :], quarters[:, 4:6, :]),
             )
 
-        raw = []
-        for b in range(B):
-            raw_b = loads.tile([P, PACK * W * H], BF16, name="raw_b")
-            nc.sync.dma_start(out=raw_b[:], in_=x[b].rearrange("(p j) w h -> p (j w h)", j=PACK))
-            raw.append(raw_b)
-            if b == 1:
-                nc.sync.dma_start(out=x3_words[:].bitcast(I32), in_=w1_words[0].bitcast(I32)[:, C : C + C // 2])
-                for to, quarters in paired(pair_words[:].bitcast(I32), w1_words[0].bitcast(I32)[:, 0:C], QUARTER // 2):
-                    nc.sync.dma_start(out=to, in_=quarters)
+        load(1)
+        nc.sync.dma_start(out=x3_words[:].bitcast(I32), in_=w1_words[0].bitcast(I32)[:, C : C + C // 2])
+        for to, quarters in paired(pair_words[:].bitcast(I32), w1_words[0].bitcast(I32)[:, 0:C], QUARTER // 2):
+            nc.sync.dma_start(out=to, in_=quarters)
+        for b in range(2, B):
+            load(b)
 
         grouped = []
         words = []
@@ -133,14 +138,22 @@ def tile_modelnew_pa_t_kernel(tc, x, w1_words, w1_scales, b1, out_0, out_1, out_
                 in_=grouped[s][:, part, :, :].rearrange("p r m j -> p (r m j)"),
             )
 
+        def row_before(b, copy):
+            by_g = grouped[b % SETS][:].rearrange("p r (w g) j -> p r w g j", g=G)
+            copy(out=by_g[:, 0, :, 1:G, :], in_=by_g[:, ROWS, :, 0 : G - 1, :])
+            copy(out=by_g[:, 0, :, 0, :], in_=by_g[:, 1, :, 0, :])
+
+        def row_after(b, copy):
+            by_g = grouped[b % SETS][:].rearrange("p r (w g) j -> p r w g j", g=G)
+            copy(out=by_g[:, ROWS + 1, :, 0 : G - 1, :], in_=by_g[:, 1, :, 1:G, :])
+            copy(out=by_g[:, ROWS + 1, :, G - 1, :], in_=by_g[:, ROWS, :, G - 1, :])
+
         def prepare(b, last_copy):
             s = b % SETS
             quantise(s, 1, ROWS)
-            by_g = grouped[s][:].rearrange("p r (w g) j -> p r w g j", g=G)
-            nc.vector.tensor_copy(out=by_g[:, 0, :, 1:G, :], in_=by_g[:, ROWS, :, 0 : G - 1, :])
-            nc.vector.tensor_copy(out=by_g[:, 0, :, 0, :], in_=by_g[:, 1, :, 0, :])
-            nc.vector.tensor_copy(out=by_g[:, ROWS + 1, :, 0 : G - 1, :], in_=by_g[:, 1, :, 1:G, :])
-            nc.vector.tensor_copy(out=by_g[:, ROWS + 1, :, G - 1, :], in_=by_g[:, ROWS, :, G - 1, :])
+            if b == 0:
+                row_before(b, nc.vector.tensor_copy)
+            row_after(b, nc.vector.tensor_copy)
             move_in_w(words[s], G, None)
             quantise(s, 0, 1)
             quantise(s, ROWS + 1, 1)
@@ -194,6 +207,7 @@ def tile_modelnew_pa_t_kernel(tc, x, w1_words, w1_scales, b1, out_0, out_1, out_
 
         for i in range(ROWS):
             regroup_columns(1, i)
+        row_before(1, nc.scalar.copy)
 
         def store(branch, b, columns, rows):
             by_partition = outs[branch][b].rearrange("w (g i) c -> (w g) (i c)", i=ROWS)
@@ -276,6 +290,8 @@ def tile_modelnew_pa_t_kernel(tc, x, w1_words, w1_scales, b1, out_0, out_1, out_
                 )
                 if b + 2 < B:
                     regroup_columns(b + 2, i)
+                    if i == ROWS - 1:
+                        row_before(b + 2, nc.scalar.copy)
                 if i == 0 and b + 1 < B:
                     prepare(b + 1, nc.gpsimd.tensor_copy)
                 if slot == ROWS_PER_STORE - 1:

@@ -47,14 +47,6 @@ def tile_modelnew_pa_t_kernel(tc, x, w1_words, w1_scales, b1, out_0, out_1, out_
         unread = ctx.enter_context(tc.tile_pool(name="unread", bufs=4))
         banks = ctx.enter_context(tc.psum_pool(name="banks", bufs=8))
 
-        x3_words = keep.tile([P, 2 * C], U8, align_bytes=64)
-        w_plane = keep.tile([P, BRANCHES * C], U8, align_bytes=64)
-        nc.gpsimd.memset(w_plane[:].bitcast(I32), 0)
-        for quadrant in range(4):
-            nc.sync.dma_start(
-                out=w_plane[32 * quadrant : 32 * quadrant + 4, :].bitcast(I32),
-                in_=w1_scales[0, 4 * quadrant : 4 * quadrant + 4, :].bitcast(I32),
-            )
         raw = []
 
         def load(b):
@@ -63,6 +55,15 @@ def tile_modelnew_pa_t_kernel(tc, x, w1_words, w1_scales, b1, out_0, out_1, out_
             raw.append(raw_b)
 
         load(0)
+
+        x3_words = keep.tile([P, 2 * C], U8, align_bytes=64)
+        w_plane = keep.tile([P, BRANCHES * C], U8, align_bytes=64)
+        nc.gpsimd.memset(w_plane[:].bitcast(I32), 0)
+        for quadrant in range(4):
+            nc.sync.dma_start(
+                out=w_plane[32 * quadrant : 32 * quadrant + 4, :].bitcast(I32),
+                in_=w1_scales[0, 4 * quadrant : 4 * quadrant + 4, :].bitcast(I32),
+            )
         bias_row = keep.tile([P, BRANCHES * C], BF16)
         nc.vector.memset(bias_row[:].bitcast(I32), 0)
         nc.sync.dma_start(out=bias_row[0:1, :], in_=b1.rearrange("(o n) -> o n", o=1))
@@ -151,9 +152,8 @@ def tile_modelnew_pa_t_kernel(tc, x, w1_words, w1_scales, b1, out_0, out_1, out_
         def prepare(b, last_copy):
             s = b % SETS
             quantise(s, 1, ROWS)
-            if b == 0:
-                row_before(b, nc.vector.tensor_copy)
-            row_after(b, nc.vector.tensor_copy)
+            if b > 0:
+                row_after(b, nc.vector.tensor_copy)
             move_in_w(words[s], G, None)
             quantise(s, 0, 1)
             quantise(s, ROWS + 1, 1)
@@ -178,15 +178,16 @@ def tile_modelnew_pa_t_kernel(tc, x, w1_words, w1_scales, b1, out_0, out_1, out_
             first = branch * C + q * QUARTER
             return source[:, 2 * at : 2 * (at + QUARTER)].bitcast(FP4X4), w_plane[:, first : first + QUARTER]
 
+        for i in range(ROWS):
+            regroup(nc.vector.tensor_copy if i < ROWS - 1 else nc.scalar.copy, 0, i)
+        row_before(0, nc.scalar.copy)
+        row_after(0, nc.scalar.copy)
+        prepare(0, None)
         for to, quarters in paired(pair_plane[:].bitcast(I32), w_plane[:].bitcast(I32)[:, 0 : C // 2], QUARTER // 4):
             nc.vector.tensor_copy(out=to, in_=quarters)
 
-        for i in range(ROWS):
-            regroup(nc.vector.tensor_copy if i < ROWS - 1 else nc.scalar.copy, 0, i)
-        prepare(0, None)
-
         bias = keep.tile([P, BRANCHES * C], F32)
-        for branch in range(BRANCHES):
+        for branch in (2, 0, 1):
             cols = slice(branch * C, (branch + 1) * C)
             spread = banks.tile([P, C], F32, name="bank")
             nc.tensor.matmul(out=spread[:], lhsT=ones[:], rhs=bias_row[:, cols], start=True, stop=True)

@@ -59,11 +59,15 @@ def tile_modelnew_pa_t_kernel(tc, x, w1_words, w1_scales, b1, out_0, out_1, out_
         x3_words = keep.tile([P, 2 * C], U8, align_bytes=64)
         w_plane = keep.tile([P, BRANCHES * C], U8, align_bytes=64)
         nc.gpsimd.memset(w_plane[:].bitcast(I32), 0)
-        for quadrant in range(4):
-            nc.sync.dma_start(
-                out=w_plane[32 * quadrant : 32 * quadrant + 4, :].bitcast(I32),
-                in_=w1_scales[0, 4 * quadrant : 4 * quadrant + 4, :].bitcast(I32),
-            )
+
+        def load_scales(quadrants):
+            for quadrant in quadrants:
+                nc.sync.dma_start(
+                    out=w_plane[32 * quadrant : 32 * quadrant + 4, :].bitcast(I32),
+                    in_=w1_scales[0, 4 * quadrant : 4 * quadrant + 4, :].bitcast(I32),
+                )
+
+        load_scales((0, 1))
         bias_row = keep.tile([P, BRANCHES * C], BF16)
         nc.vector.memset(bias_row[:].bitcast(I32), 0)
         nc.sync.dma_start(out=bias_row[0:1, :], in_=b1.rearrange("(o n) -> o n", o=1))
@@ -82,7 +86,9 @@ def tile_modelnew_pa_t_kernel(tc, x, w1_words, w1_scales, b1, out_0, out_1, out_
 
         load(1)
         nc.sync.dma_start(out=x3_words[:].bitcast(I32), in_=w1_words[0].bitcast(I32)[:, C : C + C // 2])
-        for to, quarters in paired(pair_words[:].bitcast(I32), w1_words[0].bitcast(I32)[:, 0:C], QUARTER // 2):
+        for k, (to, quarters) in enumerate(paired(pair_words[:].bitcast(I32), w1_words[0].bitcast(I32)[:, 0:C], QUARTER // 2)):
+            if k == 2:
+                load_scales((2, 3))
             nc.sync.dma_start(out=to, in_=quarters)
         for b in range(2, B):
             load(b)
@@ -114,8 +120,8 @@ def tile_modelnew_pa_t_kernel(tc, x, w1_words, w1_scales, b1, out_0, out_1, out_
             part = slice(k * P // ROWS, (k + 1) * P // ROWS)
             by_column = raw[b][:].rearrange("p (j m i) -> p j m i", j=PACK, i=ROWS)
             nc.scalar.copy(
-                out=grouped[b % SETS][:, 1 : 1 + ROWS, part, :].rearrange("p r m j -> p m j r"),
-                in_=by_column[:, :, part, :].rearrange("p j m i -> p m j i"),
+                out=grouped[b % SETS][:, 1 : 1 + ROWS, part, :].rearrange("p r (m two) j -> p m j two r", two=2),
+                in_=by_column[:, :, part, :].rearrange("p j (m two) i -> p m j two i", two=2),
             )
 
         def move_in_w(tiles, step, last_copy):

from contextlib import ExitStack

import concourse.mybir as mybir
from concourse.masks import make_identity

BF16 = mybir.dt.bfloat16
F32 = mybir.dt.float32
I32 = mybir.dt.int32
U32 = mybir.dt.uint32
U8 = mybir.dt.uint8
FP8X4 = mybir.dt.float8_e4m3fn_x4
FP4X4 = mybir.dt.float4_e2m1fn_x4
ADD = mybir.AluOpType.add
IDENTITY = mybir.ActivationFunctionType.Identity

B, C, W, H = 8, 512, 16, 32
P = 128
PACK = 4
ROWS = 4
G = H // ROWS
QUARTERS = 4
QUARTER = C // QUARTERS
PAIR = 2 * QUARTER
BRANCHES = 3
FLOPS = 2 * B * W * H * C * BRANCHES * C

SAME, W_MINUS, W_PLUS, H_MINUS, H_PLUS = 0, 1, 2, 3, 4
SHIFTS = (
    (W_MINUS, W_PLUS, H_MINUS, H_PLUS),
    (H_MINUS, H_PLUS, W_MINUS, W_PLUS),
    (SAME, SAME, SAME, SAME),
)

ROWS_PER_STORE = 2
SETS = 2
ONES_WIDTH = 32


def tile_modelnew_pa_t_kernel(tc, x, w1_words, w1_scales, b1, out_0, out_1, out_2, out_3):
    nc = tc.nc
    outs = (out_0, out_1, out_2)
    with ExitStack() as ctx:
        ctx.enter_context(tc.manual_schedule())
        keep = ctx.enter_context(tc.tile_pool(name="keep", bufs=1))
        loads = ctx.enter_context(tc.tile_pool(name="loads", bufs=B))
        results = ctx.enter_context(tc.tile_pool(name="results", bufs=4))
        unread = ctx.enter_context(tc.tile_pool(name="unread", bufs=4))
        banks = ctx.enter_context(tc.psum_pool(name="banks", bufs=8))

        raw = []

        def load(b):
            raw_b = loads.tile([P, PACK * W * H], BF16, name="raw_b")
            nc.sync.dma_start(out=raw_b[:], in_=x[b].rearrange("(p j) w h -> p (j w h)", j=PACK))
            raw.append(raw_b)

        load(0)

        x3_words = keep.tile([P, 2 * C], U8, align_bytes=64)
        w_plane = keep.tile([P, BRANCHES * C], U8, align_bytes=64)
        nc.gpsimd.memset(w_plane[:].bitcast(I32), 0)

        def load_scales(quadrants):
            for quadrant in quadrants:
                nc.sync.dma_start(
                    out=w_plane[32 * quadrant : 32 * quadrant + 4, :].bitcast(I32),
                    in_=w1_scales[0, 4 * quadrant : 4 * quadrant + 4, :].bitcast(I32),
                )

        load_scales((0, 1))
        bias_row = keep.tile([P, BRANCHES * C], BF16)
        nc.vector.memset(bias_row[:].bitcast(I32), 0)
        nc.sync.dma_start(out=bias_row[0:1, :], in_=b1.rearrange("(o n) -> o n", o=1))

        pair_words = keep.tile([P, 2 * 2 * C], U8, align_bytes=64)
        pair_plane = keep.tile([P, 2 * C], U8, align_bytes=64)

        def paired(dst, src, unit):
            to = dst.rearrange("p (s two c) -> p s two c", two=2, c=unit)
            quarters = src.rearrange("p (k c) -> p k c", c=unit)
            return (
                (to[:, :, 0, :], quarters[:, 0:4, :]),
                (to[:, 0:2, 1, :], quarters[:, 6:8, :]),
                (to[:, 2:4, 1, :], quarters[:, 4:6, :]),
            )

        load(1)
        nc.sync.dma_start(out=x3_words[:].bitcast(I32), in_=w1_words[0].bitcast(I32)[:, C : C + C // 2])
        for k, (to, quarters) in enumerate(paired(pair_words[:].bitcast(I32), w1_words[0].bitcast(I32)[:, 0:C], QUARTER // 2)):
            if k == 2:
                load_scales((2, 3))
            nc.sync.dma_start(out=to, in_=quarters)
        for b in range(2, B):
            load(b)

        grouped = []
        words = []
        planes = []
        for s in range(SETS):
            grouped.append(keep.tile([P, ROWS + 2, P, PACK], BF16, name="grouped%d" % s, align_bytes=64))
            words.append({})
            planes.append({})
            for shift, n_rows in ((SAME, ROWS + 2), (W_MINUS, ROWS), (W_PLUS, ROWS)):
                words[s][shift] = keep.tile([P, n_rows, P], U32, name="words%d_%d" % (s, shift), align_bytes=64)
                planes[s][shift] = keep.tile([P, n_rows, P], U8, name="planes%d_%d" % (s, shift), align_bytes=64)
            nc.vector.memset(planes[s][SAME][:].bitcast(I32), 0)

        ones = keep.tile([P, P], BF16)
        nc.vector.memset(ones[:], 1.0)
        a_by_channel = keep.tile([P, P], F32)
        nc.vector.memset(a_by_channel[:], 0.0)
        identity = keep.tile([P, P], F32)
        make_identity(nc, identity[:])

        def regroup(copy, b, i):
            by_row = raw[b][:].rearrange("p (j m i) -> p j m i", j=PACK, i=ROWS)
            copy(out=grouped[b % SETS][:, 1 + i, :, :], in_=by_row[:, :, :, i].rearrange("p j m -> p m j"))

        def regroup_columns(b, k):
            part = slice(k * P // ROWS, (k + 1) * P // ROWS)
            by_column = raw[b][:].rearrange("p (j m i) -> p j m i", j=PACK, i=ROWS)
            nc.scalar.copy(
                out=grouped[b % SETS][:, 1 : 1 + ROWS, part, :].rearrange("p r (m two) j -> p m j two r", two=2),
                in_=by_column[:, :, part, :].rearrange("p j (m two) i -> p m j two i", two=2),
            )

        def move_in_w(tiles, step, last_copy):
            same = tiles[SAME][:].bitcast(I32)[:, 1 : 1 + ROWS, :]
            minus = tiles[W_MINUS][:].bitcast(I32)
            plus = tiles[W_PLUS][:].bitcast(I32)
            n = same.shape[2]
            nc.vector.tensor_copy(out=minus[:, :, step:n], in_=same[:, :, 0 : n - step])
            nc.vector.tensor_copy(out=minus[:, :, 0:step], in_=same[:, :, 0:step])
            nc.vector.tensor_copy(out=plus[:, :, 0 : n - step], in_=same[:, :, step:n])
            if last_copy is None:
                nc.vector.tensor_copy(out=plus[:, :, n - step : n], in_=same[:, :, n - step : n])
            else:
                last_copy(out=plus[:, :, n - step : n], in_=plus[:, :, n - 2 * step : n - step])

        def quantise(s, first, n_rows):
            part = slice(first, first + n_rows)
            nc.vector.quantize_mx(
                out=words[s][SAME][:, part, :].rearrange("p r m -> p (r m)").bitcast(FP8X4),
                scales=planes[s][SAME][:, part, :].rearrange("p r m -> p (r m)"),
                in_=grouped[s][:, part, :, :].rearrange("p r m j -> p (r m j)"),
            )

        def row_before(b, copy):
            by_g = grouped[b % SETS][:].rearrange("p r (w g) j -> p r w g j", g=G)
            copy(out=by_g[:, 0, :, 1:G, :], in_=by_g[:, ROWS, :, 0 : G - 1, :])
            copy(out=by_g[:, 0, :, 0, :], in_=by_g[:, 1, :, 0, :])

        def row_after(b, copy):
            by_g = grouped[b % SETS][:].rearrange("p r (w g) j -> p r w g j", g=G)
            copy(out=by_g[:, ROWS + 1, :, 0 : G - 1, :], in_=by_g[:, 1, :, 1:G, :])
            copy(out=by_g[:, ROWS + 1, :, G - 1, :], in_=by_g[:, ROWS, :, G - 1, :])

        def prepare(b, last_copy):
            s = b % SETS
            quantise(s, 1, ROWS)
            if b > 0:
                row_after(b, nc.vector.tensor_copy)
            move_in_w(words[s], G, None)
            quantise(s, 0, 1)
            quantise(s, ROWS + 1, 1)
            move_in_w(planes[s], G // 4, last_copy)

        def shifted_rows(b, shift, i, n_rows):
            s = b % SETS
            if shift in (W_MINUS, W_PLUS):
                source, first = shift, i
            else:
                source, first = SAME, i + {H_MINUS: 0, SAME: 1, H_PLUS: 2}[shift]
            return (
                words[s][source][:, first : first + n_rows, :].rearrange("p r m -> p (r m)").bitcast(FP8X4),
                planes[s][source][:, first : first + n_rows, :].rearrange("p r m -> p (r m)"),
            )

        def weight_quarter(branch, q):
            if branch == BRANCHES - 1:
                source, at = x3_words, q * QUARTER
            else:
                source, at = pair_words, (2 * q if branch == 0 else 2 * ((q + 2) % QUARTERS) + 1) * QUARTER
            first = branch * C + q * QUARTER
            return source[:, 2 * at : 2 * (at + QUARTER)].bitcast(FP4X4), w_plane[:, first : first + QUARTER]

        for i in range(ROWS):
            regroup(nc.vector.tensor_copy if i < ROWS - 1 else nc.scalar.copy, 0, i)
        row_before(0, nc.scalar.copy)
        row_after(0, nc.scalar.copy)
        prepare(0, None)
        for to, quarters in paired(pair_plane[:].bitcast(I32), w_plane[:].bitcast(I32)[:, 0 : C // 2], QUARTER // 4):
            nc.vector.tensor_copy(out=to, in_=quarters)

        bias = keep.tile([P, BRANCHES * C], F32)
        for branch in (2, 0, 1):
            cols = slice(branch * C, (branch + 1) * C)
            spread = banks.tile([P, C], F32, name="bank")
            nc.tensor.matmul(out=spread[:], lhsT=ones[:], rhs=bias_row[:, cols], start=True, stop=True)
            nc.scalar.copy(out=bias[:, cols], in_=spread[:])
        bias_turned = banks.tile([P, QUARTERS, ONES_WIDTH], F32, name="bank")
        for q in range(QUARTERS):
            for branch in range(BRANCHES):
                first = branch * C + q * QUARTER
                nc.tensor.matmul(
                    out=bias_turned[:, q, :],
                    lhsT=bias_row[:, first : first + QUARTER],
                    rhs=ones[:, 0:ONES_WIDTH],
                    start=branch == 0,
                    stop=branch == BRANCHES - 1,
                )
        bias_by_channel = keep.tile([P, QUARTERS], F32)
        nc.scalar.copy(out=bias_by_channel[:], in_=bias_turned[:, :, 0])

        for i in range(ROWS):
            regroup_columns(1, i)
        row_before(1, nc.scalar.copy)

        def store(branch, b, columns, rows):
            by_partition = outs[branch][b].rearrange("w (g i) c -> (w g) (i c)", i=ROWS)
            nc.sync.dma_start(out=by_partition[:, columns], in_=rows)

        for b in range(B):
            for i in range(ROWS):
                slot = i % ROWS_PER_STORE
                if i == 0:
                    rows_x3 = results.tile([P, ROWS, C], F32, name="rows_x3", bufs=3)
                if slot == 0:
                    rows_x12 = results.tile([P, 3 * ROWS_PER_STORE * C], F32, name="rows_x12")
                bank = banks.tile([P, C], F32, name="bank")
                points, point_scales = shifted_rows(b, SAME, i, 1)
                nc.tensor.matmul_mx(
                    out=bank[:],
                    lhsT=points,
                    lhsT_scale=point_scales,
                    rhs=x3_words[:].bitcast(FP4X4),
                    rhs_scale=w_plane[:, 2 * C : 3 * C],
                    start=True,
                    stop=True,
                )
                out_row = rows_x3[:, i, :]
                bias_cols = bias[:, 2 * C : 3 * C]
                if i != (ROWS - 1 if b == B - 1 else 0):
                    nc.scalar.copy(out=out_row, in_=bank[:])
                    nc.gpsimd.tensor_tensor(out=out_row, in0=out_row, in1=bias_cols, op=ADD)
                else:
                    nc.vector.tensor_tensor(out=out_row, in0=bank[:], in1=bias_cols, op=ADD)
                for kind, shifts in enumerate(((W_MINUS, W_PLUS), (H_MINUS, H_PLUS))):
                    bank = banks.tile([P, C], F32, name="bank")
                    for s, shift in enumerate(shifts):
                        points, point_scales = shifted_rows(b, shift, i, 1)
                        first = (2 * kind + s) * PAIR
                        nc.tensor.matmul_mx(
                            out=bank[:, s * PAIR : (s + 1) * PAIR],
                            lhsT=points,
                            lhsT_scale=point_scales,
                            rhs=pair_words[:, 2 * first : 2 * (first + PAIR)].bitcast(FP4X4),
                            rhs_scale=pair_plane[:, first : first + PAIR],
                            start=True,
                            stop=True,
                        )
                    one_branch = ROWS_PER_STORE * C
                    if kind == 0:
                        at, step = slot * C, one_branch + PAIR
                        bias_view = bias[:, 0 : 3 * C].rearrange("p (br x) -> p br x", br=2)[:, :, 0:PAIR]
                    else:
                        at, step = slot * C + PAIR, one_branch - PAIR
                        bias_view = bias[:, PAIR : 3 * PAIR].rearrange("p (br x) -> p br x", br=2)
                    out_view = rows_x12[:, at : at + 2 * step].rearrange("p (br x) -> p br x", br=2)[:, :, 0:PAIR]
                    nc.vector.tensor_tensor(
                        out=out_view.rearrange("p br (s c) -> p br s c", c=QUARTER),
                        in0=bank[:].rearrange("p (s br c) -> p br s c", s=2, br=2),
                        in1=bias_view.rearrange("p br (s c) -> p br s c", c=QUARTER),
                        op=ADD,
                    )
                q = i
                bank = banks.tile([P, C], F32, name="bank")
                for branch in range(BRANCHES):
                    points, point_scales = shifted_rows(b, SHIFTS[branch][q], 0, ROWS)
                    columns, column_scales = weight_quarter(branch, q)
                    nc.tensor.matmul_mx(
                        out=bank[:],
                        lhsT=columns,
                        lhsT_scale=column_scales,
                        rhs=points,
                        rhs_scale=point_scales,
                        start=branch == 0,
                        stop=branch == BRANCHES - 1,
                    )
                with_bias = unread.tile([P, C], F32)
                nc.scalar.activation(
                    out=with_bias[:],
                    in_=bank[:],
                    func=IDENTITY,
                    bias=bias_by_channel[:, q : q + 1],
                    accum_out=a_by_channel[:, QUARTERS * b + q : QUARTERS * b + q + 1],
                )
                if b + 2 < B:
                    regroup_columns(b + 2, i)
                    if i == ROWS - 1:
                        row_before(b + 2, nc.scalar.copy)
                if i == 0 and b + 1 < B:
                    prepare(b + 1, nc.gpsimd.tensor_copy)
                if slot == ROWS_PER_STORE - 1:
                    one_branch = ROWS_PER_STORE * C
                    halves = slice((i - slot) * C, (i + 1) * C)
                    store(0, b, halves, rows_x12[:, 0:one_branch])
                    store(1, b, halves, rows_x12[:, one_branch : 2 * one_branch])
                    x3 = rows_x3[:].rearrange("p r c -> p (r c)")
                    if b in (0, B - 1):
                        store(2, b, halves, x3[:, halves])
                    elif i == ROWS - 1:
                        store(2, b, slice(0, ROWS * C), x3)

        a_turned = banks.tile([P, P], F32, name="bank")
        nc.tensor.transpose(a_turned[:], a_by_channel[:], identity[:])
        a_rows = keep.tile([P, P], F32)
        nc.scalar.copy(out=a_rows[:], in_=a_turned[:])
        nc.sync.dma_start(out=out_3.rearrange("b (q c) -> (b q) c", c=QUARTER), in_=a_rows[0 : QUARTERS * B, :])
